import numpy as np
import ml_dtypes


def mxq(x, axis, fmt="e4m3"):
    dtype, down = {"e4m3": (ml_dtypes.float8_e4m3fn, 7), "e5m2": (ml_dtypes.float8_e5m2, 14)}[fmt]
    v = np.moveaxis(np.asarray(x, np.float32).astype(ml_dtypes.bfloat16).astype(np.float64), axis, -1)
    blocks = v.reshape(v.shape[:-1] + (-1, 32))
    amax = np.abs(blocks).max(-1, keepdims=True)
    byte = np.maximum(np.where(amax > 0, np.frexp(amax)[1] - 1 + 127, 0) - down, 1)
    scale = np.exp2(byte - 127.0)
    codes = (blocks / scale).astype(np.float32).astype(dtype).astype(np.float64)
    return np.moveaxis((codes * scale).reshape(v.shape), -1, axis)


WIDE = False


def mx_kscale(k):
    if not WIDE:
        return np.ones(k)
    levels = np.array([10, -10, 5, -5, 0])
    if k % 512:
        return np.exp2(np.random.permutation(np.resize(levels, k // 32))).repeat(32)
    a = np.empty((k // 512, 16))
    for p in range(k // 512):
        a[p, :8] = np.random.permutation(np.resize(levels, 8))
        for g in range(8):
            far = levels[np.abs(levels - a[p, g]) >= 10]
            a[p, g + 8] = far[np.random.randint(len(far))]
    return np.exp2(a.ravel()).repeat(32)


BF16 = ml_dtypes.bfloat16


def bf(x):
    return np.asarray(x, np.float32).astype(BF16)


def f64(x):
    return np.asarray(x).astype(np.float64)


B, N, D, F1, F2, F3, G1, G2 = 4, 32, 512, 512, 1024, 512, 512, 512
ALPHA = 0.2


def lrelu(v):
    return np.maximum(v, ALPHA * v)


def draw0():
    s, t = mx_kscale(D), mx_kscale(F1)
    ss = np.concatenate([s, s])
    return {"x": bf(np.random.standard_normal((B, N, D)) * s),
            "fe_w0": bf(np.random.standard_normal((D + D, F1)) / np.sqrt(D + D) / ss[:, None] * t),
            "fe_b0": bf(np.random.standard_normal(F1) * 0.3 * t),
            "fe_w1": bf(np.random.standard_normal((F1, F2)) * 1.4 / np.sqrt(F1) / t[:, None]),
            "fe_b1": bf(np.random.standard_normal(F2) * 0.3)}


def core(x, fe_w0, fe_b0, fe_w1, fe_b1):
    xq = mxq(f64(x), 2, "e4m3")
    w0 = f64(fe_w0)
    u = xq @ mxq(w0[:D], 0, "e4m3")
    v = xq @ mxq(w0[D:], 0, "e4m3")
    e1 = lrelu(u[:, :, None, :] + v[:, None, :, :] + f64(fe_b0))
    return lrelu((mxq(e1, 3, "e4m3") @ mxq(f64(fe_w1), 0, "e4m3")) + f64(fe_b1))


def e4m3fn_bytes(y):
    return np.clip(np.asarray(y, np.float64), -448.0, 448.0).astype(np.float32).astype(ml_dtypes.float8_e4m3fn).view(np.uint8)


def e4m3fn_values(b):
    return np.asarray(b, np.uint8).view(ml_dtypes.float8_e4m3fn).astype(np.float64)


def setup_inputs():
    d = draw0()
    x0 = np.asarray(d['fe_w1']).astype(np.float64)
    s = (np.max(np.abs(x0), axis=(1,), keepdims=True) / 448.0).astype(np.float32)
    out = {}
    for k, v in d.items():
        if k == 'fe_w1':
            out['fe_w1_bytes'] = e4m3fn_bytes(x0 / s.astype(np.float64))
            out['fe_w1_scale'] = s
        else:
            out[k] = v
    return out


def reference(x, fe_w0, fe_b0, fe_w1_bytes, fe_w1_scale, fe_b1):
    return core(x, fe_w0, fe_b0, e4m3fn_values(fe_w1_bytes) * fe_w1_scale.astype(np.float64), fe_b1)

@@ -1,0 +1,280 @@
+from contextlib import ExitStack
+
+import concourse.mybir as mybir
+from concourse.masks import make_identity
+
+F32 = mybir.dt.float32
+BF16 = mybir.dt.bfloat16
+U32 = mybir.dt.uint32
+U8 = mybir.dt.uint8
+FP8 = mybir.dt.float8_e4m3fn
+FP8X4 = mybir.dt.float8_e4m3fn_x4
+ALU = mybir.AluOpType
+ACT = mybir.ActivationFunctionType
+
+P = 128
+FLOPS = 2 * 128 * 512 * 512 * 2 + 2 * 4096 * 512 * 1024
+ALPHA = 0.2
+CHUNKS = 8
+TOK = 512
+
+
+def tile_graph_gan_pa_kernel(tc, x, fe_w0, fe_b0, fe_w1_bytes, fe_w1_scale, fe_b1, out):
+    nc = tc.nc
+    rows = out.rearrange("b i j c -> (b i j) c")
+
+    with ExitStack() as ctx:
+        keep = ctx.enter_context(tc.tile_pool(name="keep", bufs=1))
+        work = ctx.enter_context(tc.tile_pool(name="work", bufs=2))
+        psum = ctx.enter_context(tc.psum_pool(name="psum", bufs=4))
+        ctx.enter_context(tc.manual_schedule())
+
+        x_sb = keep.tile([P, 512], BF16, name="x_sb", align_bytes=64)
+        w0_raw = [keep.tile([P, 4, 512], BF16, name="w0_raw%d" % h, align_bytes=64) for h in range(2)]
+        w1_bytes = keep.tile([P, 4096], U8, name="w1_bytes", align_bytes=64)
+        w1_scale = keep.tile([P, 4], F32, name="w1_scale")
+        b0_sb = keep.tile([P, 4], BF16, name="b0_sb")
+        b1_rows = keep.tile([P, P], BF16, name="b1_rows")
+        b1_bc = keep.tile([P, P], BF16, name="b1_bc")
+        nc.sync.dma_start(out=x_sb[:], in_=x.rearrange("b n d -> (b n) d"))
+        for h in range(2):
+            nc.sync.dma_start(out=w0_raw[h][:], in_=fe_w0[512 * h : 512 * h + 512, :].rearrange("(p j) w -> p j w", j=4))
+        nc.sync.dma_start(out=w1_bytes[:], in_=fe_w1_bytes.rearrange("(p t) n -> p (t n)", t=4))
+        nc.scalar.dma_start(out=w1_scale[:], in_=fe_w1_scale.rearrange("(p t) o -> p (t o)", t=4))
+        nc.scalar.dma_start(out=b0_sb[:], in_=fe_b0.rearrange("(p t) -> p t", t=4))
+
+        ident = keep.tile([P, P], F32, name="ident")
+        identb = keep.tile([P, P], BF16, name="identb")
+        warm = keep.tile([P, 8], F32, name="warm")
+        nc.gpsimd.memset(warm[:], 0.0)
+        nc.gpsimd.memset(b1_rows[:], 0.0)
+        make_identity(nc, ident[:])
+        make_identity(nc, identb[:])
+        nc.scalar.dma_start(out=b1_rows[0:8, :], in_=fe_b1.rearrange("(c m) -> c m", m=P))
+        nc.scalar.dma_start(out=b1_bc[:], in_=fe_b1[896:1024].partition_broadcast(P))
+        nc.scalar.activation(out=warm[:], in_=warm[:], func=ACT.Identity, bias=0.0, scale=1.0)
+
+        xw = x_sb[:].bitcast(F32)
+        xt = psum.tile([P, 2, P], F32, name="xt", tag="mm")
+        for u in range(2):
+            nc.tensor.transpose(xt[:, u, :], xw[:, u:256:2], ident[:])
+        xg = keep.tile([P, P, 4], BF16, name="xg", align_bytes=64)
+        nc.vector.tensor_copy(out=xg[:].rearrange("p n t -> p (n t)").bitcast(F32).rearrange("p (n u) -> p n u", u=2), in_=xt[:].rearrange("p u n -> p n u"))
+
+        w0_g = [keep.tile([P, 2048], BF16, name="w0_g%d" % h, align_bytes=64) for h in range(2)]
+        w0_c = [keep.tile([P, 512], U32, name="w0_c%d" % h, align_bytes=64) for h in range(2)]
+        w0_s = [keep.tile([P, 512], U8, name="w0_s%d" % h, align_bytes=64) for h in range(2)]
+
+        def lay_w0(copy, h, t0, t1):
+            copy(
+                out=w0_g[h][:].rearrange("p (t m j) -> p t m j", t=4, j=4)[:, t0:t1],
+                in_=w0_raw[h][:].rearrange("p j (m t) -> p t m j", t=4)[:, t0:t1],
+            )
+
+        x_c = keep.tile([P, P], U32, name="x_c", align_bytes=64)
+        x_s = keep.tile([P, P], U8, name="x_s", align_bytes=64)
+        lay_w0(nc.vector.tensor_copy, 0, 0, 2)
+        lay_w0(nc.scalar.copy, 0, 2, 4)
+        nc.vector.quantize_mx(out=x_c[:].bitcast(FP8X4), scales=x_s[:], in_=xg[:].rearrange("p n t -> p (n t)"))
+        lay_w0(nc.vector.tensor_copy, 1, 0, 2)
+        nc.vector.quantize_mx(out=w0_c[0][:].bitcast(FP8X4), scales=w0_s[0][:], in_=w0_g[0][:])
+        lay_w0(nc.scalar.copy, 1, 2, 4)
+        nc.vector.quantize_mx(out=w0_c[1][:].bitcast(FP8X4), scales=w0_s[1][:], in_=w0_g[1][:])
+
+        uv = []
+        for h in range(2):
+            acc = psum.tile([P, 4, P], F32, name="uv%d" % h, tag="mm")
+            for t in range(4):
+                nc.tensor.matmul_mx(
+                    out=acc[:, t, :],
+                    lhsT=w0_c[h][:, 128 * t : 128 * t + 128].bitcast(FP8X4),
+                    lhsT_scale=w0_s[h][:, 128 * t : 128 * t + 128],
+                    rhs=x_c[:].bitcast(FP8X4),
+                    rhs_scale=x_s[:],
+                    start=True,
+                    stop=True,
+                )
+            uv.append(acc)
+        u_sb = keep.tile([P, P, 4], F32, name="u_sb")
+        v_sb = keep.tile([P, P, 4], F32, name="v_sb")
+        nc.scalar.copy(out=u_sb[:], in_=uv[0][:].rearrange("p t n -> p n t"))
+        nc.vector.tensor_tensor(out=v_sb[:], in0=uv[1][:].rearrange("p t n -> p n t"), in1=b0_sb[:].unsqueeze(1).to_broadcast([P, P, 4]), op=ALU.add)
+
+        w1_p = keep.tile([P, 4, 1024], BF16, name="w1_p", align_bytes=64)
+        w1_g = keep.tile([P, 1024, 4], BF16, name="w1_g", align_bytes=64)
+        w1_c = keep.tile([P, 1024], U32, name="w1_c", align_bytes=64)
+        w1_s = keep.tile([P, 1024], U8, name="w1_s", align_bytes=64)
+        for t in range(4):
+            nc.scalar.activation(
+                out=w1_p[:, t, :],
+                in_=w1_bytes[:, 1024 * t : 1024 * t + 1024].bitcast(FP8),
+                func=ACT.Copy,
+                scale=w1_scale[:, t : t + 1],
+            )
+        for q in range(2):
+            nc.scalar.copy(out=w1_g[:, 512 * q : 512 * q + 512, :], in_=w1_p[:, :, 512 * q : 512 * q + 512].rearrange("p t n -> p n t"))
+        b1_t = psum.tile([P, P], BF16, name="b1_t", tag="tp")
+        nc.tensor.transpose(b1_t[:], b1_rows[:], identb[:])
+        b1_a = keep.tile([P, 8], F32, name="b1_a")
+        nc.scalar.activation(out=b1_a[:], in_=b1_t[:, 0:8], func=ACT.Copy, scale=ALPHA)
+
+        zpre = {}
+        e1 = {}
+        codes = {}
+
+        def e1_add(k, g):
+            b, i0 = k // 2, 16 * (k % 2) + 8 * g
+            z = work.tile([P, 8, 32, 4], F32, name="zpre", tag="zpre", bufs=3)
+            nc.vector.tensor_tensor(
+                out=z[:],
+                in0=u_sb[:, 32 * b + i0 : 32 * b + i0 + 8, :].unsqueeze(2).to_broadcast([P, 8, 32, 4]),
+                in1=v_sb[:, 32 * b : 32 * b + 32, :].unsqueeze(1).to_broadcast([P, 8, 32, 4]),
+                op=ALU.add,
+            )
+            zpre[k, g] = z
+
+        def e1_lrelu(k, g):
+            if g == 0:
+                e1[k] = work.tile([P, 2048], BF16, name="e1", tag="e1", align_bytes=64)
+            z = zpre[k, g][:].rearrange("p i j t -> p (i j t)")
+            nc.vector.scalar_tensor_tensor(out=e1[k][:, 1024 * g : 1024 * g + 1024], in0=z, scalar=ALPHA, in1=z, op0=ALU.mult, op1=ALU.max)
+
+        def e1_quant(k):
+            c = work.tile([P, TOK], U32, name="e1_c", tag="e1_c", bufs=3, align_bytes=64)
+            s = work.tile([P, TOK], U8, name="e1_s", tag="e1_s", bufs=3, align_bytes=64)
+            nc.vector.quantize_mx(out=c[:].bitcast(FP8X4), scales=s[:], in_=e1[k][:])
+            codes[k] = (c, s)
+
+        rounds = [(k, h) for k in range(CHUNKS) for h in range(2)]
+
+        def ctiles(r):
+            return [0, 1, 2, 3] if rounds[r][1] == 0 else [4, 5, 6]
+
+        pt = {}
+        at = {}
+        rt = {}
+        o_sb = {}
+        p1 = {}
+        zp = {}
+
+        def mx(r, i):
+            k = rounds[r][0]
+            c = ctiles(r)[i]
+            acc = psum.tile([P, TOK], F32, name="pt", tag="mm")
+            nc.tensor.matmul_mx(
+                out=acc[:],
+                lhsT=w1_c[:, 128 * c : 128 * c + 128].bitcast(FP8X4),
+                lhsT_scale=w1_s[:, 128 * c : 128 * c + 128],
+                rhs=codes[k][0][:].bitcast(FP8X4),
+                rhs_scale=codes[k][1][:],
+                start=True,
+                stop=True,
+            )
+            pt[r, i] = acc
+
+        def mx_tok(k):
+            acc = psum.tile([P, 4, P], F32, name="p1", tag="mm")
+            for s in range(4):
+                nc.tensor.matmul_mx(
+                    out=acc[:, s, :],
+                    lhsT=codes[k][0][:, 128 * s : 128 * s + 128].bitcast(FP8X4),
+                    lhsT_scale=codes[k][1][:, 128 * s : 128 * s + 128],
+                    rhs=w1_c[:, 896:1024].bitcast(FP8X4),
+                    rhs_scale=w1_s[:, 896:1024],
+                    start=True,
+                    stop=True,
+                )
+            p1[k] = acc
+
+        def p1_add(k):
+            z = work.tile([P, 4, P], F32, name="zp", tag="zp")
+            nc.vector.tensor_tensor(out=z[:], in0=p1[k][:], in1=b1_bc[:].unsqueeze(1).to_broadcast([P, 4, P]), op=ALU.add)
+            zp[k] = z
+
+        def p1_lrelu(k):
+            nc.vector.scalar_tensor_tensor(out=o_sb[k, 1][:, :, 384:512], in0=zp[k][:], scalar=ALPHA, in1=zp[k][:], op0=ALU.mult, op1=ALU.max)
+
+        def lin(r, i):
+            if i == 0:
+                at[r] = work.tile([P, 4, TOK], F32, name="at", tag="at", bufs=3)
+                rt[r] = work.tile([P, 4, TOK], F32, name="rt", tag="rt", bufs=3)
+                o_sb[rounds[r]] = work.tile([P, 4, TOK], F32, name="o_sb%d" % rounds[r][1], tag="o_sb%d" % rounds[r][1])
+            c = ctiles(r)[i]
+            nc.scalar.activation(out=at[r][:, i, :], in_=pt[r, i][:], func=ACT.Identity, bias=b1_a[:, c : c + 1], scale=ALPHA)
+
+        def relu(r, i):
+            nc.vector.tensor_scalar(out=rt[r][:, i, :], in0=at[r][:, i, :], scalar1=4.0, scalar2=0.0, op0=ALU.mult, op1=ALU.max)
+
+        tp = {}
+
+        def turn(r, s):
+            acc = psum.tile([P, TOK], F32, name="tp", tag="tp")
+            for i in range(len(ctiles(r))):
+                for n, src in enumerate((at[r], rt[r])):
+                    nc.tensor.matmul(
+                        acc[:, 128 * i : 128 * i + 128],
+                        lhsT=src[:, i, 128 * s : 128 * s + 128],
+                        rhs=ident[:],
+                        is_transpose=True,
+                        start=(n == 0),
+                        stop=(n == 1),
+                    )
+            tp[r, s] = acc
+
+        def leave(r, s):
+            k, h = rounds[r]
+            w = 128 * len(ctiles(r))
+            if r >= 14 and s % 2 == 1:
+                nc.vector.tensor_copy(out=o_sb[k, h][:, s, 0:w], in_=tp[r, s][:, 0:w])
+            else:
+                nc.scalar.copy(out=o_sb[k, h][:, s, 0:w], in_=tp[r, s][:, 0:w])
+            r0 = TOK * k + 128 * s
+            nc.sync.dma_start(out=rows[r0 : r0 + 128, 512 * h : 512 * h + 512], in_=o_sb[k, h][:, s, :])
+
+        e1_add(0, 0)
+        e1_add(0, 1)
+        e1_lrelu(0, 0)
+        nc.vector.quantize_mx(out=w1_c[:, 0:512].bitcast(FP8X4), scales=w1_s[:, 0:512], in_=w1_g[:, 0:512, :].rearrange("p n t -> p (n t)"))
+        e1_lrelu(0, 1)
+        nc.vector.quantize_mx(out=w1_c[:, 512:1024].bitcast(FP8X4), scales=w1_s[:, 512:1024], in_=w1_g[:, 512:1024, :].rearrange("p n t -> p (n t)"))
+        e1_quant(0)
+        for i in range(4):
+            mx(0, i)
+        e1_add(1, 0)
+        e1_add(1, 1)
+
+        nr = len(rounds)
+        for r in range(nr + 1):
+            k, h = rounds[r] if r < nr else (CHUNKS, 0)
+            more = k + 1 < CHUNKS
+            for i in range(4):
+                slot = 4 * h + i
+                if r < nr and i < len(ctiles(r)):
+                    lin(r, i)
+                if more:
+                    if slot == 0:
+                        e1_lrelu(k + 1, 0)
+                    elif slot == 2:
+                        e1_lrelu(k + 1, 1)
+                    elif slot == 4:
+                        e1_quant(k + 1)
+                if k + 2 < CHUNKS:
+                    if slot == 5:
+                        e1_add(k + 2, 0)
+                    elif slot == 7:
+                        e1_add(k + 2, 1)
+                if r < nr and slot == 6:
+                    p1_add(k)
+                if r < nr and slot == 7:
+                    p1_lrelu(k)
+                if r < nr and i < len(ctiles(r)):
+                    relu(r, i)
+                if r > 0:
+                    turn(r - 1, i)
+                    leave(r - 1, i)
+                if i % 2 == 1 and r + 1 < nr:
+                    for m in (i - 1, i):
+                        if m < len(ctiles(r + 1)):
+                            mx(r + 1, m)
+                        else:
+                            mx_tok(k)

@@ -50,8 +50,8 @@ def tile_graph_gan_pa_kernel(tc, x, fe_w0, fe_b0, fe_w1_bytes, fe_w1_scale, fe_b
         nc.gpsimd.memset(b1_rows[:], 0.0)
         make_identity(nc, ident[:])
         make_identity(nc, identb[:])
-        nc.scalar.dma_start(out=b1_rows[0:8, :], in_=fe_b1.rearrange("(c m) -> c m", m=P))
-        nc.scalar.dma_start(out=b1_bc[:], in_=fe_b1[896:1024].partition_broadcast(P))
+        nc.sync.dma_start(out=b1_rows[0:8, :], in_=fe_b1.rearrange("(c m) -> c m", m=P))
+        nc.sync.dma_start(out=b1_bc[:], in_=fe_b1[896:1024].partition_broadcast(P))
         nc.scalar.activation(out=warm[:], in_=warm[:], func=ACT.Identity, bias=0.0, scale=1.0)
 
         xw = x_sb[:].bitcast(F32)
@@ -81,6 +81,33 @@ def tile_graph_gan_pa_kernel(tc, x, fe_w0, fe_b0, fe_w1_bytes, fe_w1_scale, fe_b
         lay_w0(nc.scalar.copy, 1, 2, 4)
         nc.vector.quantize_mx(out=w0_c[1][:].bitcast(FP8X4), scales=w0_s[1][:], in_=w0_g[1][:])
 
+        w1_p = keep.tile([P, 4, 1024], BF16, name="w1_p", align_bytes=64)
+        w1_g = keep.tile([P, 1024, 4], BF16, name="w1_g", align_bytes=64)
+        w1_c = keep.tile([P, 1024], U32, name="w1_c", align_bytes=64)
+        w1_s = keep.tile([P, 1024], U8, name="w1_s", align_bytes=64)
+
+        def w1_widen(q, t):
+            n0 = 512 * q
+            nc.scalar.activation(
+                out=w1_p[:, t, n0 : n0 + 512],
+                in_=w1_bytes[:, 1024 * t + n0 : 1024 * t + n0 + 512].bitcast(FP8),
+                func=ACT.Copy,
+                scale=w1_scale[:, t : t + 1],
+            )
+
+        def w1_lay(copy, n0, n1):
+            copy(out=w1_g[:, n0:n1, :], in_=w1_p[:, :, n0:n1].rearrange("p t n -> p n t"))
+
+        def w1_quant(q):
+            n0 = 512 * q
+            nc.vector.quantize_mx(
+                out=w1_c[:, n0 : n0 + 512].bitcast(FP8X4),
+                scales=w1_s[:, n0 : n0 + 512],
+                in_=w1_g[:, n0 : n0 + 512, :].rearrange("p n t -> p (n t)"),
+            )
+
+        w1_widen(0, 0)
+        w1_widen(0, 1)
         uv = []
         for h in range(2):
             acc = psum.tile([P, 4, P], F32, name="uv%d" % h, tag="mm")
@@ -99,20 +126,11 @@ def tile_graph_gan_pa_kernel(tc, x, fe_w0, fe_b0, fe_w1_bytes, fe_w1_scale, fe_b
         v_sb = keep.tile([P, P, 4], F32, name="v_sb")
         nc.scalar.copy(out=u_sb[:], in_=uv[0][:].rearrange("p t n -> p n t"))
         nc.vector.tensor_tensor(out=v_sb[:], in0=uv[1][:].rearrange("p t n -> p n t"), in1=b0_sb[:].unsqueeze(1).to_broadcast([P, P, 4]), op=ALU.add)
-
-        w1_p = keep.tile([P, 4, 1024], BF16, name="w1_p", align_bytes=64)
-        w1_g = keep.tile([P, 1024, 4], BF16, name="w1_g", align_bytes=64)
-        w1_c = keep.tile([P, 1024], U32, name="w1_c", align_bytes=64)
-        w1_s = keep.tile([P, 1024], U8, name="w1_s", align_bytes=64)
+        w1_widen(0, 2)
+        w1_widen(0, 3)
+        w1_lay(nc.scalar.copy, 0, 512)
         for t in range(4):
-            nc.scalar.activation(
-                out=w1_p[:, t, :],
-                in_=w1_bytes[:, 1024 * t : 1024 * t + 1024].bitcast(FP8),
-                func=ACT.Copy,
-                scale=w1_scale[:, t : t + 1],
-            )
-        for q in range(2):
-            nc.scalar.copy(out=w1_g[:, 512 * q : 512 * q + 512, :], in_=w1_p[:, :, 512 * q : 512 * q + 512].rearrange("p t n -> p n t"))
+            w1_widen(1, t)
         b1_t = psum.tile([P, P], BF16, name="b1_t", tag="tp")
         nc.tensor.transpose(b1_t[:], b1_rows[:], identb[:])
         b1_a = keep.tile([P, 8], F32, name="b1_a")
@@ -196,14 +214,14 @@ def tile_graph_gan_pa_kernel(tc, x, fe_w0, fe_b0, fe_w1_bytes, fe_w1_scale, fe_b
 
         def lin(r, i):
             if i == 0:
-                at[r] = work.tile([P, 4, TOK], F32, name="at", tag="at", bufs=3)
-                rt[r] = work.tile([P, 4, TOK], F32, name="rt", tag="rt", bufs=3)
+                at[r] = work.tile([P, 4, TOK], F32, name="at", tag="at", bufs=4)
+                rt[r] = work.tile([P, 4, TOK], F32, name="rt", tag="rt", bufs=4)
                 o_sb[rounds[r]] = work.tile([P, 4, TOK], F32, name="o_sb%d" % rounds[r][1], tag="o_sb%d" % rounds[r][1])
             c = ctiles(r)[i]
             nc.scalar.activation(out=at[r][:, i, :], in_=pt[r, i][:], func=ACT.Identity, bias=b1_a[:, c : c + 1], scale=ALPHA)
 
-        def relu(r, i):
-            nc.vector.tensor_scalar(out=rt[r][:, i, :], in0=at[r][:, i, :], scalar1=4.0, scalar2=0.0, op0=ALU.mult, op1=ALU.max)
+        def relu(r, i0, i1):
+            nc.vector.tensor_scalar(out=rt[r][:, i0:i1, :], in0=at[r][:, i0:i1, :], scalar1=4.0, scalar2=0.0, op0=ALU.mult, op1=ALU.max)
 
         tp = {}
 
@@ -234,47 +252,50 @@ def tile_graph_gan_pa_kernel(tc, x, fe_w0, fe_b0, fe_w1_bytes, fe_w1_scale, fe_b
         e1_add(0, 0)
         e1_add(0, 1)
         e1_lrelu(0, 0)
-        nc.vector.quantize_mx(out=w1_c[:, 0:512].bitcast(FP8X4), scales=w1_s[:, 0:512], in_=w1_g[:, 0:512, :].rearrange("p n t -> p (n t)"))
+        w1_quant(0)
         e1_lrelu(0, 1)
-        nc.vector.quantize_mx(out=w1_c[:, 512:1024].bitcast(FP8X4), scales=w1_s[:, 512:1024], in_=w1_g[:, 512:1024, :].rearrange("p n t -> p (n t)"))
+        w1_lay(nc.vector.tensor_copy, 512, 1024)
         e1_quant(0)
+        w1_quant(1)
         for i in range(4):
             mx(0, i)
-        e1_add(1, 0)
-        e1_add(1, 1)
+
+        pieces = []
+        for k in range(1, CHUNKS):
+            pieces += [(e1_add, k, 0), (e1_add, k, 1), (e1_lrelu, k, 0), (e1_lrelu, k, 1), (e1_quant, k)]
+
+        def due(g):
+            if g < 4:
+                return g + 2
+            if g < 10:
+                return 5 + (5 * (g - 3)) // 6
+            return 10 + (5 * (g - 9)) // 8
 
         nr = len(rounds)
-        for r in range(nr + 1):
+        done = 0
+        for r in range(nr + 2):
             k, h = rounds[r] if r < nr else (CHUNKS, 0)
-            more = k + 1 < CHUNKS
             for i in range(4):
-                slot = 4 * h + i
                 if r < nr and i < len(ctiles(r)):
                     lin(r, i)
-                if more:
-                    if slot == 0:
-                        e1_lrelu(k + 1, 0)
-                    elif slot == 2:
-                        e1_lrelu(k + 1, 1)
-                    elif slot == 4:
-                        e1_quant(k + 1)
-                if k + 2 < CHUNKS:
-                    if slot == 5:
-                        e1_add(k + 2, 0)
-                    elif slot == 7:
-                        e1_add(k + 2, 1)
-                if r < nr and slot == 6:
+                while done < min(due(4 * r + i), len(pieces)):
+                    pieces[done][0](*pieces[done][1:])
+                    done += 1
+                if r < nr and h == 1 and i == 2:
                     p1_add(k)
-                if r < nr and slot == 7:
+                if r < nr and i % 2 == 1:
+                    relu(r, i - 1, min(i + 1, len(ctiles(r))))
+                if r < nr and h == 1 and i == 3:
                     p1_lrelu(k)
-                if r < nr and i < len(ctiles(r)):
-                    relu(r, i)
-                if r > 0:
-                    turn(r - 1, i)
-                    leave(r - 1, i)
-                if i % 2 == 1 and r + 1 < nr:
-                    for m in (i - 1, i):
-                        if m < len(ctiles(r + 1)):
-                            mx(r + 1, m)
-                        else:
-                            mx_tok(k)
+                if r > 1:
+                    leave(r - 2, i)
+                if i % 2 == 1:
+                    if 0 < r <= nr:
+                        turn(r - 1, i - 1)
+                        turn(r - 1, i)
+                    if r + 1 < nr:
+                        for m in (i - 1, i):
+                            if m < len(ctiles(r + 1)):
+                                mx(r + 1, m)
+                            else:
+                                mx_tok(k)

@@ -17,6 +17,20 @@ FLOPS = 2 * 128 * 512 * 512 * 2 + 2 * 4096 * 512 * 1024
 ALPHA = 0.2
 CHUNKS = 8
 TOK = 512
+NP = (0, 1, 0, 1, 0, 1, 2, 3)
+COLAG = 6
+ELEAD = 2.0
+P1LAG = 0
+VLAG = 12
+MXLEAD = 4
+STICK = 3
+HOP = 50
+SAME = 200
+V0 = 0
+S0 = 0
+WKEY = 3
+UKEY = 1
+LKEY = 3
 
 
 def tile_graph_gan_pa_kernel(tc, x, fe_w0, fe_b0, fe_w1_bytes, fe_w1_scale, fe_b1, out):
@@ -35,10 +49,11 @@ def tile_graph_gan_pa_kernel(tc, x, fe_w0, fe_b0, fe_w1_bytes, fe_w1_scale, fe_b
         w1_scale = keep.tile([P, 4], F32, name="w1_scale")
         b0_sb = keep.tile([P, 4], BF16, name="b0_sb")
         b1_rows = keep.tile([P, P], BF16, name="b1_rows")
-        b1_bc = keep.tile([P, P], BF16, name="b1_bc")
-        nc.sync.dma_start(out=x_sb[:], in_=x.rearrange("b n d -> (b n) d"))
-        for h in range(2):
+        b1_bc = keep.tile([P, 512], BF16, name="b1_bc")
+        for h in (1, 0):
             nc.sync.dma_start(out=w0_raw[h][:], in_=fe_w0[512 * h : 512 * h + 512, :].rearrange("(p j) w -> p j w", j=4))
+            if h == 1:
+                nc.sync.dma_start(out=x_sb[:], in_=x.rearrange("b n d -> (b n) d"))
         nc.sync.dma_start(out=w1_bytes[:], in_=fe_w1_bytes.rearrange("(p t) n -> p (t n)", t=4))
         nc.scalar.dma_start(out=w1_scale[:], in_=fe_w1_scale.rearrange("(p t) o -> p (t o)", t=4))
         nc.scalar.dma_start(out=b0_sb[:], in_=fe_b0.rearrange("(p t) -> p t", t=4))
@@ -51,7 +66,7 @@ def tile_graph_gan_pa_kernel(tc, x, fe_w0, fe_b0, fe_w1_bytes, fe_w1_scale, fe_b
         make_identity(nc, ident[:])
         make_identity(nc, identb[:])
         nc.sync.dma_start(out=b1_rows[0:8, :], in_=fe_b1.rearrange("(c m) -> c m", m=P))
-        nc.sync.dma_start(out=b1_bc[:], in_=fe_b1[896:1024].partition_broadcast(P))
+        nc.sync.dma_start(out=b1_bc[:], in_=fe_b1[512:1024].partition_broadcast(P))
         nc.scalar.activation(out=warm[:], in_=warm[:], func=ACT.Identity, bias=0.0, scale=1.0)
 
         xw = x_sb[:].bitcast(F32)
@@ -59,7 +74,7 @@ def tile_graph_gan_pa_kernel(tc, x, fe_w0, fe_b0, fe_w1_bytes, fe_w1_scale, fe_b
         for u in range(2):
             nc.tensor.transpose(xt[:, u, :], xw[:, u:256:2], ident[:])
         xg = keep.tile([P, P, 4], BF16, name="xg", align_bytes=64)
-        nc.vector.tensor_copy(out=xg[:].rearrange("p n t -> p (n t)").bitcast(F32).rearrange("p (n u) -> p n u", u=2), in_=xt[:].rearrange("p u n -> p n u"))
+        xg_copy = dict(out=xg[:].rearrange("p n t -> p (n t)").bitcast(F32).rearrange("p (n u) -> p n u", u=2), in_=xt[:].rearrange("p u n -> p n u"))
 
         w0_g = [keep.tile([P, 2048], BF16, name="w0_g%d" % h, align_bytes=64) for h in range(2)]
         w0_c = [keep.tile([P, 512], U32, name="w0_c%d" % h, align_bytes=64) for h in range(2)]
@@ -71,15 +86,16 @@ def tile_graph_gan_pa_kernel(tc, x, fe_w0, fe_b0, fe_w1_bytes, fe_w1_scale, fe_b
                 in_=w0_raw[h][:].rearrange("p j (m t) -> p t m j", t=4)[:, t0:t1],
             )
 
+        lay_w0(nc.vector.tensor_copy, 1, 0, 2)
+        nc.vector.tensor_copy(**xg_copy)
         x_c = keep.tile([P, P], U32, name="x_c", align_bytes=64)
         x_s = keep.tile([P, P], U8, name="x_s", align_bytes=64)
-        lay_w0(nc.vector.tensor_copy, 0, 0, 2)
-        lay_w0(nc.scalar.copy, 0, 2, 4)
-        nc.vector.quantize_mx(out=x_c[:].bitcast(FP8X4), scales=x_s[:], in_=xg[:].rearrange("p n t -> p (n t)"))
-        lay_w0(nc.vector.tensor_copy, 1, 0, 2)
-        nc.vector.quantize_mx(out=w0_c[0][:].bitcast(FP8X4), scales=w0_s[0][:], in_=w0_g[0][:])
         lay_w0(nc.scalar.copy, 1, 2, 4)
+        nc.vector.quantize_mx(out=x_c[:].bitcast(FP8X4), scales=x_s[:], in_=xg[:].rearrange("p n t -> p (n t)"))
+        lay_w0(nc.vector.tensor_copy, 0, 0, 2)
         nc.vector.quantize_mx(out=w0_c[1][:].bitcast(FP8X4), scales=w0_s[1][:], in_=w0_g[1][:])
+        lay_w0(nc.scalar.copy, 0, 2, 4)
+        nc.vector.quantize_mx(out=w0_c[0][:].bitcast(FP8X4), scales=w0_s[0][:], in_=w0_g[0][:])
 
         w1_p = keep.tile([P, 4, 1024], BF16, name="w1_p", align_bytes=64)
         w1_g = keep.tile([P, 1024, 4], BF16, name="w1_g", align_bytes=64)
@@ -98,18 +114,16 @@ def tile_graph_gan_pa_kernel(tc, x, fe_w0, fe_b0, fe_w1_bytes, fe_w1_scale, fe_b
         def w1_lay(copy, n0, n1):
             copy(out=w1_g[:, n0:n1, :], in_=w1_p[:, :, n0:n1].rearrange("p t n -> p n t"))
 
-        def w1_quant(q):
-            n0 = 512 * q
+        def w1_quant(n0, n1):
             nc.vector.quantize_mx(
-                out=w1_c[:, n0 : n0 + 512].bitcast(FP8X4),
-                scales=w1_s[:, n0 : n0 + 512],
-                in_=w1_g[:, n0 : n0 + 512, :].rearrange("p n t -> p (n t)"),
+                out=w1_c[:, n0:n1].bitcast(FP8X4),
+                scales=w1_s[:, n0:n1],
+                in_=w1_g[:, n0:n1, :].rearrange("p n t -> p (n t)"),
             )
 
         w1_widen(0, 0)
-        w1_widen(0, 1)
-        uv = []
-        for h in range(2):
+        uv = {}
+        for h in (1, 0):
             acc = psum.tile([P, 4, P], F32, name="uv%d" % h, tag="mm")
             for t in range(4):
                 nc.tensor.matmul_mx(
@@ -121,20 +135,30 @@ def tile_graph_gan_pa_kernel(tc, x, fe_w0, fe_b0, fe_w1_bytes, fe_w1_scale, fe_b
                     start=True,
                     stop=True,
                 )
-            uv.append(acc)
+            uv[h] = acc
         u_sb = keep.tile([P, P, 4], F32, name="u_sb")
         v_sb = keep.tile([P, P, 4], F32, name="v_sb")
-        nc.scalar.copy(out=u_sb[:], in_=uv[0][:].rearrange("p t n -> p n t"))
-        nc.vector.tensor_tensor(out=v_sb[:], in0=uv[1][:].rearrange("p t n -> p n t"), in1=b0_sb[:].unsqueeze(1).to_broadcast([P, P, 4]), op=ALU.add)
-        w1_widen(0, 2)
-        w1_widen(0, 3)
-        w1_lay(nc.scalar.copy, 0, 512)
-        for t in range(4):
-            w1_widen(1, t)
+
+        def u_leave(n0, n1):
+            nc.scalar.copy(out=u_sb[:, n0:n1, :], in_=uv[0][:, :, n0:n1].rearrange("p t n -> p n t"))
+
+        def v_leave(n0, n1):
+            nc.vector.tensor_tensor(
+                out=v_sb[:, n0:n1, :],
+                in0=uv[1][:, :, n0:n1].rearrange("p t n -> p n t"),
+                in1=b0_sb[:].unsqueeze(1).to_broadcast([P, n1 - n0, 4]),
+                op=ALU.add,
+            )
+
+        v_leave(0, 32)
+        w1_widen(0, 1)
+        u_leave(0, 32)
         b1_t = psum.tile([P, P], BF16, name="b1_t", tag="tp")
         nc.tensor.transpose(b1_t[:], b1_rows[:], identb[:])
         b1_a = keep.tile([P, 8], F32, name="b1_a")
-        nc.scalar.activation(out=b1_a[:], in_=b1_t[:, 0:8], func=ACT.Copy, scale=ALPHA)
+
+        def b1_leave():
+            nc.scalar.activation(out=b1_a[:], in_=b1_t[:, 0:8], func=ACT.Copy, scale=ALPHA)
 
         zpre = {}
         e1 = {}
@@ -157,145 +181,197 @@ def tile_graph_gan_pa_kernel(tc, x, fe_w0, fe_b0, fe_w1_bytes, fe_w1_scale, fe_b
             z = zpre[k, g][:].rearrange("p i j t -> p (i j t)")
             nc.vector.scalar_tensor_tensor(out=e1[k][:, 1024 * g : 1024 * g + 1024], in0=z, scalar=ALPHA, in1=z, op0=ALU.mult, op1=ALU.max)
 
-        def e1_quant(k):
-            c = work.tile([P, TOK], U32, name="e1_c", tag="e1_c", bufs=3, align_bytes=64)
-            s = work.tile([P, TOK], U8, name="e1_s", tag="e1_s", bufs=3, align_bytes=64)
-            nc.vector.quantize_mx(out=c[:].bitcast(FP8X4), scales=s[:], in_=e1[k][:])
-            codes[k] = (c, s)
+        def e1_quant(k, g0, g1):
+            if g0 == 0:
+                codes[k] = (
+                    work.tile([P, TOK], U32, name="e1_c", tag="e1_c", bufs=4, align_bytes=64),
+                    work.tile([P, TOK], U8, name="e1_s", tag="e1_s", bufs=4, align_bytes=64),
+                )
+            c, s = codes[k]
+            t0, t1 = 256 * g0, 256 * g1
+            nc.vector.quantize_mx(out=c[:, t0:t1].bitcast(FP8X4), scales=s[:, t0:t1], in_=e1[k][:, 4 * t0 : 4 * t1])
 
-        rounds = [(k, h) for k in range(CHUNKS) for h in range(2)]
-
-        def ctiles(r):
-            return [0, 1, 2, 3] if rounds[r][1] == 0 else [4, 5, 6]
-
-        pt = {}
+        acc = {}
         at = {}
         rt = {}
-        o_sb = {}
-        p1 = {}
         zp = {}
+        tp = {}
 
-        def mx(r, i):
-            k = rounds[r][0]
-            c = ctiles(r)[i]
-            acc = psum.tile([P, TOK], F32, name="pt", tag="mm")
-            nc.tensor.matmul_mx(
-                out=acc[:],
-                lhsT=w1_c[:, 128 * c : 128 * c + 128].bitcast(FP8X4),
-                lhsT_scale=w1_s[:, 128 * c : 128 * c + 128],
-                rhs=codes[k][0][:].bitcast(FP8X4),
-                rhs_scale=codes[k][1][:],
-                start=True,
-                stop=True,
-            )
-            pt[r, i] = acc
+        def is_tok(n):
+            return n % 8 >= 8 - NP[n // 8]
 
-        def mx_tok(k):
-            acc = psum.tile([P, 4, P], F32, name="p1", tag="mm")
-            for s in range(4):
+        def mx(n, t0, t1):
+            k, c = n // 8, n % 8
+            if t0 == 0:
+                acc[n] = psum.tile([P, TOK], F32, name="acc", tag="mm")
+            w_cols = slice(128 * c, 128 * c + 128)
+            if is_tok(n):
+                for s in range(4):
+                    nc.tensor.matmul_mx(
+                        out=acc[n][:, 128 * s : 128 * s + 128],
+                        lhsT=codes[k][0][:, 128 * s : 128 * s + 128].bitcast(FP8X4),
+                        lhsT_scale=codes[k][1][:, 128 * s : 128 * s + 128],
+                        rhs=w1_c[:, w_cols].bitcast(FP8X4),
+                        rhs_scale=w1_s[:, w_cols],
+                        start=True,
+                        stop=True,
+                    )
+            else:
                 nc.tensor.matmul_mx(
-                    out=acc[:, s, :],
-                    lhsT=codes[k][0][:, 128 * s : 128 * s + 128].bitcast(FP8X4),
-                    lhsT_scale=codes[k][1][:, 128 * s : 128 * s + 128],
-                    rhs=w1_c[:, 896:1024].bitcast(FP8X4),
-                    rhs_scale=w1_s[:, 896:1024],
+                    out=acc[n][:, t0:t1],
+                    lhsT=w1_c[:, w_cols].bitcast(FP8X4),
+                    lhsT_scale=w1_s[:, w_cols],
+                    rhs=codes[k][0][:, t0:t1].bitcast(FP8X4),
+                    rhs_scale=codes[k][1][:, t0:t1],
                     start=True,
                     stop=True,
                 )
-            p1[k] = acc
 
-        def p1_add(k):
-            z = work.tile([P, 4, P], F32, name="zp", tag="zp")
-            nc.vector.tensor_tensor(out=z[:], in0=p1[k][:], in1=b1_bc[:].unsqueeze(1).to_broadcast([P, 4, P]), op=ALU.add)
-            zp[k] = z
+        def tok_add(n):
+            c = n % 8
+            zp[n] = work.tile([P, 4, P], F32, name="zp", tag="zp", bufs=3)
+            nc.vector.tensor_tensor(
+                out=zp[n][:],
+                in0=acc[n][:].rearrange("p (s c) -> p s c", s=4),
+                in1=b1_bc[:, 128 * c - 512 : 128 * c - 384].unsqueeze(1).to_broadcast([P, 4, P]),
+                op=ALU.add,
+            )
 
-        def p1_lrelu(k):
-            nc.vector.scalar_tensor_tensor(out=o_sb[k, 1][:, :, 384:512], in0=zp[k][:], scalar=ALPHA, in1=zp[k][:], op0=ALU.mult, op1=ALU.max)
+        def tok_lrelu(n):
+            k, c = n // 8, n % 8
+            o = work.tile([P, 4, P], F32, name="tok_o", tag="tok_o", bufs=3)
+            nc.vector.scalar_tensor_tensor(out=o[:], in0=zp[n][:], scalar=ALPHA, in1=zp[n][:], op0=ALU.mult, op1=ALU.max)
+            nc.sync.dma_start(out=rows[TOK * k : TOK * k + TOK, 128 * c : 128 * c + 128].rearrange("(s p) c -> p s c", p=P), in_=o[:])
 
-        def lin(r, i):
-            if i == 0:
-                at[r] = work.tile([P, 4, TOK], F32, name="at", tag="at", bufs=4)
-                rt[r] = work.tile([P, 4, TOK], F32, name="rt", tag="rt", bufs=4)
-                o_sb[rounds[r]] = work.tile([P, 4, TOK], F32, name="o_sb%d" % rounds[r][1], tag="o_sb%d" % rounds[r][1])
-            c = ctiles(r)[i]
-            nc.scalar.activation(out=at[r][:, i, :], in_=pt[r, i][:], func=ACT.Identity, bias=b1_a[:, c : c + 1], scale=ALPHA)
+        def lin(n, t0, t1):
+            half, i = n // 4, n % 4
+            if i == 0 and t0 == 0:
+                at[half] = work.tile([P, 4, TOK], F32, name="at", tag="at", bufs=4)
+                rt[half] = work.tile([P, 4, TOK], F32, name="rt", tag="rt", bufs=4)
+            c = n % 8
+            nc.scalar.activation(out=at[half][:, i, t0:t1], in_=acc[n][:, t0:t1], func=ACT.Identity, bias=b1_a[:, c : c + 1], scale=ALPHA)
 
-        def relu(r, i0, i1):
-            nc.vector.tensor_scalar(out=rt[r][:, i0:i1, :], in0=at[r][:, i0:i1, :], scalar1=4.0, scalar2=0.0, op0=ALU.mult, op1=ALU.max)
+        def relu(half, i0, i1):
+            nc.vector.tensor_scalar(out=rt[half][:, i0:i1, :], in0=at[half][:, i0:i1, :], scalar1=4.0, scalar2=0.0, op0=ALU.mult, op1=ALU.max)
 
-        tp = {}
+        def tiles(half):
+            return 4 if half % 2 == 0 else 4 - NP[half // 2]
 
-        def turn(r, s):
-            acc = psum.tile([P, TOK], F32, name="tp", tag="tp")
-            for i in range(len(ctiles(r))):
-                for n, src in enumerate((at[r], rt[r])):
+        def turn(m):
+            half, s = m // 4, m % 4
+            tp[m] = psum.tile([P, TOK], F32, name="tp", tag="tp")
+            for i in range(tiles(half)):
+                for q, src in enumerate((at[half], rt[half])):
                     nc.tensor.matmul(
-                        acc[:, 128 * i : 128 * i + 128],
+                        tp[m][:, 128 * i : 128 * i + 128],
                         lhsT=src[:, i, 128 * s : 128 * s + 128],
                         rhs=ident[:],
                         is_transpose=True,
-                        start=(n == 0),
-                        stop=(n == 1),
+                        start=(q == 0),
+                        stop=(q == 1),
                     )
-            tp[r, s] = acc
 
-        def leave(r, s):
-            k, h = rounds[r]
-            w = 128 * len(ctiles(r))
-            if r >= 14 and s % 2 == 1:
-                nc.vector.tensor_copy(out=o_sb[k, h][:, s, 0:w], in_=tp[r, s][:, 0:w])
+        def leave(copy, m):
+            half, s = m // 4, m % 4
+            w = 128 * tiles(half)
+            o = work.tile([P, TOK], F32, name="o", tag="o", bufs=8)
+            copy(out=o[:, 0:w], in_=tp[m][:, 0:w])
+            r0, c0 = TOK * (half // 2) + 128 * s, 512 * (half % 2)
+            nc.sync.dma_start(out=rows[r0 : r0 + 128, c0 : c0 + w], in_=o[:, 0:w])
+
+        def half_tiles(n):
+            return n // 4, n % 4
+
+        lay_s, lay_v = nc.scalar.copy, nc.vector.tensor_copy
+        streams = {}
+
+        def item(stream, name, eng, cost, deps, fn, *args):
+            streams.setdefault(stream, []).append((name, eng, cost, deps, fn, args))
+
+        for k in range(CHUNKS):
+            key = {"V": 8 * k - ELEAD}
+            parts = [("add", 0), ("lre", 0), ("q", 0), ("add", 1), ("lre", 1), ("q", 1)] if k == 0 else [("add", 0), ("add", 1), ("lre", 0), ("lre", 1), ("q", 1)]
+            for kind, g in parts:
+                if kind == "add":
+                    j = 2 * k + g - 3
+                    deps = ([("lre", j // 2, j % 2)] if j >= 0 else []) + (["v_rest", "u_rest"] if k >= 2 else [])
+                    item("e", ("add", k, g), key, 1040, deps, e1_add, k, g)
+                elif kind == "lre":
+                    deps = [("add", k, g)] + ([("q", k - 2, 1)] if k >= 2 else [])
+                    item("e", ("lre", k, g), key, 1040, deps, e1_lrelu, k, g)
+                else:
+                    deps = [("lre", k, g)] + ([("mx", 8 * (k - 4) + 7, 1)] if k >= 4 else [])
+                    item("e", ("q", k, g), key, 560 if k else 290, deps, e1_quant, k, g if k == 0 else 0, g + 1)
+
+        for t in (2, 3):
+            item("w", ("wid", 0, t), {"S": -20}, 530, [], w1_widen, 0, t)
+        item("w", "lay0", {"S": -19}, 1180, [("wid", 0, 3)], w1_lay, lay_s, 0, 256)
+        item("w", "lay1", {"S": -19}, 1180, [("wid", 0, 3)], w1_lay, lay_s, 256, 512)
+        item("w", "b1", {"S": -19}, 30, [], b1_leave)
+        for t in range(4):
+            item("w", ("wid", 1, t), {"S": WKEY}, 530, [], w1_widen, 1, t)
+        item("w", "u_rest", {"S": UKEY}, 340, [], u_leave, 32, 128)
+        item("x", "wq0", {"V": -8}, 290, ["lay0"], w1_quant, 0, 256)
+        item("x", "wq1", {"V": -8}, 290, ["lay1"], w1_quant, 256, 512)
+        item("x", "lay2", {"V": LKEY}, 1280, [("wid", 1, 3)], w1_lay, lay_v, 512, 1024)
+        item("x", "wq2", {"V": LKEY}, 560, ["lay2"], w1_quant, 512, 1024)
+        item("v", "v_rest", {"V": UKEY}, 340, [], v_leave, 32, 128)
+
+        for n in range(64):
+            k = n // 8
+            half, i = n // 4, n % 4
+            kind = "tok" if is_tok(n) else "lin"
+            for g in (0, 1) if n < 4 else (1,):
+                t0, t1 = (256 * g, 256 * g + 256) if n < 4 else (0, 512)
+                deps = [("q", k, g), "wq0" if n < 2 else "wq1" if n < 4 else "wq2"]
+                if n >= 4:
+                    deps.append(("tok" if is_tok(n - 4) else "lin", n - 4, 1))
+                if n < 4 and g == 1:
+                    deps.append(("lin", n, 0))
+                key = {"T": n - MXLEAD + (2 * g if n < 4 else 0)}
+                item("mx%d" % (g if n < 4 else 1), ("mx", n, g), key, 300 if kind == "tok" else 130 if n < 4 else 265, deps, mx, n, t0, t1)
+                if kind == "lin":
+                    deps = [("mx", n, g), "b1"] + ([("turn", 4 * half - 13)] if half >= 4 and i == 0 else [])
+                    item("lin%d" % (g if n < 4 else 1), ("lin", n, g), {"S": n + (2 * g if n < 4 else 0)}, 280 if n < 4 else 530, deps, lin, n, t0, t1)
+            if kind == "tok":
+                item("tok", ("tok", n, 1), {"V": n + P1LAG}, 530, [("mx", n, 1)], tok_add, n)
+                item("tok", ("tokl", n), {"V": n + P1LAG}, 530, [("tok", n, 1)], tok_lrelu, n)
+        for half in range(16):
+            w = tiles(half)
+            for i in range(0, w, 2):
+                j = min(i + 2, w)
+                item("relu", ("relu", half, j), {"V": 4 * half + j}, 20 + 256 * (j - i), [("lin", 4 * half + j - 1, 1)], relu, half, i, j)
+            for s in range(4):
+                m = 4 * half + s
+                item("turn", ("turn", m), {"T": m}, 160 * w, [("relu", half, w)] + ([("leave", m - 4)] if m >= 4 else []), turn, m)
+                item("leave", ("leave", m), {"S": m + COLAG, "V": m + VLAG}, 20 + 128 * w, [("turn", m)], leave, m)
+
+        end = {}
+        ran = {}
+        clock = {"V": V0, "S": S0, "T": 0}
+        last = None
+        while any(streams.values()):
+            best = None
+            for st, queue in streams.items():
+                if not queue:
+                    continue
+                name, engs, cost, deps, fn, args = queue[0]
+                if not all(d in end for d in deps):
+                    continue
+                for e, key in engs.items():
+                    start = max([clock[e]] + [end[d] + (SAME if ran[d] == e else HOP) for d in deps])
+                    rank = (start, key - (STICK if e == "T" and st[:2] == last else 0))
+                    if best is None or (e == best[1] and rank < best[0]) or (e != best[1] and start < best[0][0]):
+                        best = (rank, e, st)
+            rank, e, st = best
+            name, engs, cost, deps, fn, args = streams[st].pop(0)
+            if fn is leave:
+                fn(nc.scalar.copy if e == "S" else nc.vector.tensor_copy, *args)
             else:
-                nc.scalar.copy(out=o_sb[k, h][:, s, 0:w], in_=tp[r, s][:, 0:w])
-            r0 = TOK * k + 128 * s
-            nc.sync.dma_start(out=rows[r0 : r0 + 128, 512 * h : 512 * h + 512], in_=o_sb[k, h][:, s, :])
-
-        e1_add(0, 0)
-        e1_add(0, 1)
-        e1_lrelu(0, 0)
-        w1_quant(0)
-        e1_lrelu(0, 1)
-        w1_lay(nc.vector.tensor_copy, 512, 1024)
-        e1_quant(0)
-        w1_quant(1)
-        for i in range(4):
-            mx(0, i)
-
-        pieces = []
-        for k in range(1, CHUNKS):
-            pieces += [(e1_add, k, 0), (e1_add, k, 1), (e1_lrelu, k, 0), (e1_lrelu, k, 1), (e1_quant, k)]
-
-        def due(g):
-            if g < 4:
-                return g + 2
-            if g < 10:
-                return 5 + (5 * (g - 3)) // 6
-            return 10 + (5 * (g - 9)) // 8
-
-        nr = len(rounds)
-        done = 0
-        for r in range(nr + 2):
-            k, h = rounds[r] if r < nr else (CHUNKS, 0)
-            for i in range(4):
-                if r < nr and i < len(ctiles(r)):
-                    lin(r, i)
-                while done < min(due(4 * r + i), len(pieces)):
-                    pieces[done][0](*pieces[done][1:])
-                    done += 1
-                if r < nr and h == 1 and i == 2:
-                    p1_add(k)
-                if r < nr and i % 2 == 1:
-                    relu(r, i - 1, min(i + 1, len(ctiles(r))))
-                if r < nr and h == 1 and i == 3:
-                    p1_lrelu(k)
-                if r > 1:
-                    leave(r - 2, i)
-                if i % 2 == 1:
-                    if 0 < r <= nr:
-                        turn(r - 1, i - 1)
-                        turn(r - 1, i)
-                    if r + 1 < nr:
-                        for m in (i - 1, i):
-                            if m < len(ctiles(r + 1)):
-                                mx(r + 1, m)
-                            else:
-                                mx_tok(k)
+                fn(*args)
+            clock[e] = rank[0] + cost
+            if e == "T":
+                clock[e] += 100 if last is not None and last != st[:2] else 0
+                last = st[:2]
+            end[name] = clock[e]
+            ran[name] = e

@@ -13,24 +13,31 @@ ALU = mybir.AluOpType
 ACT = mybir.ActivationFunctionType
 
 P = 128
-FLOPS = 2 * 128 * 512 * 512 * 2 + 2 * 4096 * 512 * 1024
-ALPHA = 0.2
+NODES = 128
+PACK = 4
+K = P * PACK
+F2 = 1024
+PAIRS = 512
 CHUNKS = 8
-TOK = 512
-NP = (0, 1, 0, 1, 0, 1, 2, 3)
-COLAG = 6
-ELEAD = 2.0
-P1LAG = 0
-VLAG = 12
-MXLEAD = 4
-STICK = 3
-HOP = 50
-SAME = 200
-V0 = 0
-S0 = 0
-WKEY = 3
-UKEY = 1
-LKEY = 3
+TILES = 8
+SLOPE = 0.2
+
+FLOPS = 2 * NODES * K * K * 2 + 2 * CHUNKS * PAIRS * K * F2
+
+PAIR_TILES = (0, 1, 1, 0, 1, 1, 2, 3)
+
+E1_AHEAD = 3.0
+MX_AHEAD = 6.0
+LEAVE_S = 6.0
+LEAVE_V = 13.0
+STAY = 1.0
+FIRST = -20.0
+SOON = 2.0
+HOP = 75
+AGAIN = 250
+TURN = 80
+SWITCH = 50
+S_BUSY = 530
 
 
 def tile_graph_gan_pa_kernel(tc, x, fe_w0, fe_b0, fe_w1_bytes, fe_w1_scale, fe_b1, out):
@@ -43,335 +50,353 @@ def tile_graph_gan_pa_kernel(tc, x, fe_w0, fe_b0, fe_w1_bytes, fe_w1_scale, fe_b
         psum = ctx.enter_context(tc.psum_pool(name="psum", bufs=4))
         ctx.enter_context(tc.manual_schedule())
 
-        x_sb = keep.tile([P, 512], BF16, name="x_sb", align_bytes=64)
-        w0_raw = [keep.tile([P, 4, 512], BF16, name="w0_raw%d" % h, align_bytes=64) for h in range(2)]
-        w1_bytes = keep.tile([P, 4096], U8, name="w1_bytes", align_bytes=64)
-        w1_scale = keep.tile([P, 4], F32, name="w1_scale")
-        b0_sb = keep.tile([P, 4], BF16, name="b0_sb")
+        w0_raw = [keep.tile([P, PACK, K], BF16, name="w0_raw%d" % h, align_bytes=64) for h in range(2)]
+        x_sb = keep.tile([NODES, K], BF16, name="x_sb", align_bytes=64)
+        w1_bytes = keep.tile([P, PACK * F2], U8, name="w1_bytes", align_bytes=64)
+        w1_scale = keep.tile([P, PACK], F32, name="w1_scale")
+        b0_sb = keep.tile([P, PACK], BF16, name="b0_sb")
         b1_rows = keep.tile([P, P], BF16, name="b1_rows")
-        b1_bc = keep.tile([P, 512], BF16, name="b1_bc")
-        for h in (1, 0):
-            nc.sync.dma_start(out=w0_raw[h][:], in_=fe_w0[512 * h : 512 * h + 512, :].rearrange("(p j) w -> p j w", j=4))
-            if h == 1:
-                nc.sync.dma_start(out=x_sb[:], in_=x.rearrange("b n d -> (b n) d"))
-        nc.sync.dma_start(out=w1_bytes[:], in_=fe_w1_bytes.rearrange("(p t) n -> p (t n)", t=4))
-        nc.scalar.dma_start(out=w1_scale[:], in_=fe_w1_scale.rearrange("(p t) o -> p (t o)", t=4))
-        nc.scalar.dma_start(out=b0_sb[:], in_=fe_b0.rearrange("(p t) -> p t", t=4))
+        b1_wide = keep.tile([P, F2 // 2], BF16, name="b1_wide")
+
+        def load_w0(h):
+            nc.sync.dma_start(out=w0_raw[h][:], in_=fe_w0[K * h : K * h + K, :].rearrange("(p j) w -> p j w", j=PACK))
+
+        load_w0(1)
+        nc.sync.dma_start(out=x_sb[:], in_=x.rearrange("b n d -> (b n) d"))
+        load_w0(0)
+        nc.sync.dma_start(out=w1_bytes[:], in_=fe_w1_bytes.rearrange("(p t) n -> p (t n)", t=PACK))
+        nc.scalar.dma_start(out=w1_scale[:], in_=fe_w1_scale.rearrange("(p t) o -> p (t o)", t=PACK))
+        nc.scalar.dma_start(out=b0_sb[:], in_=fe_b0.rearrange("(p t) -> p t", t=PACK))
 
         ident = keep.tile([P, P], F32, name="ident")
-        identb = keep.tile([P, P], BF16, name="identb")
+        ident_bf16 = keep.tile([P, P], BF16, name="ident_bf16")
         warm = keep.tile([P, 8], F32, name="warm")
         nc.gpsimd.memset(warm[:], 0.0)
         nc.gpsimd.memset(b1_rows[:], 0.0)
         make_identity(nc, ident[:])
-        make_identity(nc, identb[:])
-        nc.sync.dma_start(out=b1_rows[0:8, :], in_=fe_b1.rearrange("(c m) -> c m", m=P))
-        nc.sync.dma_start(out=b1_bc[:], in_=fe_b1[512:1024].partition_broadcast(P))
+        make_identity(nc, ident_bf16[:])
+        nc.sync.dma_start(out=b1_rows[0:TILES, :], in_=fe_b1.rearrange("(c m) -> c m", m=P))
+        nc.sync.dma_start(out=b1_wide[:], in_=fe_b1[F2 // 2 : F2].partition_broadcast(P))
         nc.scalar.activation(out=warm[:], in_=warm[:], func=ACT.Identity, bias=0.0, scale=1.0)
 
-        xw = x_sb[:].bitcast(F32)
-        xt = psum.tile([P, 2, P], F32, name="xt", tag="mm")
-        for u in range(2):
-            nc.tensor.transpose(xt[:, u, :], xw[:, u:256:2], ident[:])
-        xg = keep.tile([P, P, 4], BF16, name="xg", align_bytes=64)
-        xg_copy = dict(out=xg[:].rearrange("p n t -> p (n t)").bitcast(F32).rearrange("p (n u) -> p n u", u=2), in_=xt[:].rearrange("p u n -> p n u"))
+        x_words = x_sb[:].bitcast(F32)
+        x_turned = psum.tile([P, 2, NODES], F32, name="x_turned", tag="product")
+        for w in range(2):
+            nc.tensor.transpose(x_turned[:, w, :], x_words[:, w : K // 2 : 2], ident[:])
+        x_laid = keep.tile([P, NODES, PACK], BF16, name="x_laid", align_bytes=64)
+        x_codes = keep.tile([P, NODES], U32, name="x_codes", align_bytes=64)
+        x_scales = keep.tile([P, NODES], U8, name="x_scales", align_bytes=64)
 
-        w0_g = [keep.tile([P, 2048], BF16, name="w0_g%d" % h, align_bytes=64) for h in range(2)]
-        w0_c = [keep.tile([P, 512], U32, name="w0_c%d" % h, align_bytes=64) for h in range(2)]
-        w0_s = [keep.tile([P, 512], U8, name="w0_s%d" % h, align_bytes=64) for h in range(2)]
+        w0_laid = [keep.tile([P, K * PACK], BF16, name="w0_laid%d" % h, align_bytes=64) for h in range(2)]
+        w0_codes = [keep.tile([P, K], U32, name="w0_codes%d" % h, align_bytes=64) for h in range(2)]
+        w0_scales = [keep.tile([P, K], U8, name="w0_scales%d" % h, align_bytes=64) for h in range(2)]
 
         def lay_w0(copy, h, t0, t1):
             copy(
-                out=w0_g[h][:].rearrange("p (t m j) -> p t m j", t=4, j=4)[:, t0:t1],
-                in_=w0_raw[h][:].rearrange("p j (m t) -> p t m j", t=4)[:, t0:t1],
+                out=w0_laid[h][:].rearrange("p (t m j) -> p t m j", t=PACK, j=PACK)[:, t0:t1],
+                in_=w0_raw[h][:].rearrange("p j (m t) -> p t m j", t=PACK)[:, t0:t1],
             )
 
-        lay_w0(nc.vector.tensor_copy, 1, 0, 2)
-        nc.vector.tensor_copy(**xg_copy)
-        x_c = keep.tile([P, P], U32, name="x_c", align_bytes=64)
-        x_s = keep.tile([P, P], U8, name="x_s", align_bytes=64)
+        def quant_w0(h):
+            nc.vector.quantize_mx(out=w0_codes[h][:].bitcast(FP8X4), scales=w0_scales[h][:], in_=w0_laid[h][:])
+
         lay_w0(nc.scalar.copy, 1, 2, 4)
-        nc.vector.quantize_mx(out=x_c[:].bitcast(FP8X4), scales=x_s[:], in_=xg[:].rearrange("p n t -> p (n t)"))
+        lay_w0(nc.vector.tensor_copy, 1, 0, 2)
+        nc.vector.tensor_copy(
+            out=x_laid[:].rearrange("p n t -> p (n t)").bitcast(F32).rearrange("p (n w) -> p n w", w=2),
+            in_=x_turned[:].rearrange("p w n -> p n w"),
+        )
+        nc.vector.quantize_mx(out=x_codes[:].bitcast(FP8X4), scales=x_scales[:], in_=x_laid[:].rearrange("p n t -> p (n t)"))
         lay_w0(nc.vector.tensor_copy, 0, 0, 2)
-        nc.vector.quantize_mx(out=w0_c[1][:].bitcast(FP8X4), scales=w0_s[1][:], in_=w0_g[1][:])
+        quant_w0(1)
         lay_w0(nc.scalar.copy, 0, 2, 4)
-        nc.vector.quantize_mx(out=w0_c[0][:].bitcast(FP8X4), scales=w0_s[0][:], in_=w0_g[0][:])
+        quant_w0(0)
 
-        w1_p = keep.tile([P, 4, 1024], BF16, name="w1_p", align_bytes=64)
-        w1_g = keep.tile([P, 1024, 4], BF16, name="w1_g", align_bytes=64)
-        w1_c = keep.tile([P, 1024], U32, name="w1_c", align_bytes=64)
-        w1_s = keep.tile([P, 1024], U8, name="w1_s", align_bytes=64)
+        w1_wide = keep.tile([P, PACK, F2], BF16, name="w1_wide", align_bytes=64)
+        w1_laid = keep.tile([P, F2, PACK], BF16, name="w1_laid", align_bytes=64)
+        w1_codes = keep.tile([P, F2], U32, name="w1_codes", align_bytes=64)
+        w1_scales = keep.tile([P, F2], U8, name="w1_scales", align_bytes=64)
 
-        def w1_widen(q, t):
-            n0 = 512 * q
-            nc.scalar.activation(
-                out=w1_p[:, t, n0 : n0 + 512],
-                in_=w1_bytes[:, 1024 * t + n0 : 1024 * t + n0 + 512].bitcast(FP8),
-                func=ACT.Copy,
-                scale=w1_scale[:, t : t + 1],
+        def widen_w1(e, t, n0, n1):
+            data = w1_bytes[:, F2 * t + n0 : F2 * t + n1].bitcast(FP8)
+            scale = w1_scale[:, t : t + 1]
+            if e == "S":
+                nc.scalar.activation(out=w1_wide[:, t, n0:n1], in_=data, func=ACT.Copy, scale=scale)
+            else:
+                nc.vector.tensor_scalar(out=w1_wide[:, t, n0:n1], in0=data, scalar1=scale, scalar2=None, op0=ALU.mult)
+
+        def lay_w1(e, n0, n1):
+            nc.scalar.copy(
+                out=w1_laid[:, n0:n1, :].rearrange("p (c i) t -> p c t i", i=4),
+                in_=w1_wide[:, :, n0:n1].rearrange("p t (c i) -> p c t i", i=4),
             )
 
-        def w1_lay(copy, n0, n1):
-            copy(out=w1_g[:, n0:n1, :], in_=w1_p[:, :, n0:n1].rearrange("p t n -> p n t"))
-
-        def w1_quant(n0, n1):
+        def quant_w1(e, n0, n1):
             nc.vector.quantize_mx(
-                out=w1_c[:, n0:n1].bitcast(FP8X4),
-                scales=w1_s[:, n0:n1],
-                in_=w1_g[:, n0:n1, :].rearrange("p n t -> p (n t)"),
+                out=w1_codes[:, n0:n1].bitcast(FP8X4),
+                scales=w1_scales[:, n0:n1],
+                in_=w1_laid[:, n0:n1, :].rearrange("p n t -> p (n t)"),
             )
 
-        w1_widen(0, 0)
+        u_sb = keep.tile([P, NODES, PACK], F32, name="u_sb")
+        v_sb = keep.tile([P, NODES, PACK], F32, name="v_sb")
         uv = {}
-        for h in (1, 0):
-            acc = psum.tile([P, 4, P], F32, name="uv%d" % h, tag="mm")
-            for t in range(4):
+
+        def first_layer(h):
+            uv[h] = psum.tile([P, PACK, NODES], F32, name="uv", tag="product")
+            for t in range(PACK):
                 nc.tensor.matmul_mx(
-                    out=acc[:, t, :],
-                    lhsT=w0_c[h][:, 128 * t : 128 * t + 128].bitcast(FP8X4),
-                    lhsT_scale=w0_s[h][:, 128 * t : 128 * t + 128],
-                    rhs=x_c[:].bitcast(FP8X4),
-                    rhs_scale=x_s[:],
+                    out=uv[h][:, t, :],
+                    lhsT=w0_codes[h][:, P * t : P * t + P].bitcast(FP8X4),
+                    lhsT_scale=w0_scales[h][:, P * t : P * t + P],
+                    rhs=x_codes[:].bitcast(FP8X4),
+                    rhs_scale=x_scales[:],
                     start=True,
                     stop=True,
                 )
-            uv[h] = acc
-        u_sb = keep.tile([P, P, 4], F32, name="u_sb")
-        v_sb = keep.tile([P, P, 4], F32, name="v_sb")
 
-        def u_leave(n0, n1):
+        def leave_u(e, n0, n1):
             nc.scalar.copy(out=u_sb[:, n0:n1, :], in_=uv[0][:, :, n0:n1].rearrange("p t n -> p n t"))
 
-        def v_leave(n0, n1):
+        def leave_v(e, n0, n1):
             nc.vector.tensor_tensor(
                 out=v_sb[:, n0:n1, :],
                 in0=uv[1][:, :, n0:n1].rearrange("p t n -> p n t"),
-                in1=b0_sb[:].unsqueeze(1).to_broadcast([P, n1 - n0, 4]),
+                in1=b0_sb[:].unsqueeze(1).to_broadcast([P, n1 - n0, PACK]),
                 op=ALU.add,
             )
 
-        v_leave(0, 32)
-        w1_widen(0, 1)
-        u_leave(0, 32)
-        b1_t = psum.tile([P, P], BF16, name="b1_t", tag="tp")
-        nc.tensor.transpose(b1_t[:], b1_rows[:], identb[:])
-        b1_a = keep.tile([P, 8], F32, name="b1_a")
+        widen_w1("S", 0, 0, F2 // 2)
+        first_layer(1)
+        first_layer(0)
+        leave_v("V", 0, 32)
+        widen_w1("S", 1, 0, F2 // 2)
+        leave_u("S", 0, 32)
 
-        def b1_leave():
-            nc.scalar.activation(out=b1_a[:], in_=b1_t[:, 0:8], func=ACT.Copy, scale=ALPHA)
+        b1_turned = psum.tile([P, P], BF16, name="b1_turned", tag="turned")
+        nc.tensor.transpose(b1_turned[:], b1_rows[:], ident_bf16[:])
+        b1_cols = keep.tile([P, TILES], F32, name="b1_cols")
 
-        zpre = {}
+        def leave_b1(e):
+            nc.scalar.activation(out=b1_cols[:], in_=b1_turned[:, 0:TILES], func=ACT.Copy, scale=SLOPE)
+
+        sums = {}
         e1 = {}
         codes = {}
+        scales = {}
 
-        def e1_add(k, g):
-            b, i0 = k // 2, 16 * (k % 2) + 8 * g
-            z = work.tile([P, 8, 32, 4], F32, name="zpre", tag="zpre", bufs=3)
+        def add_uv(e, k, g):
+            graph, i0 = k // 2, 32 * (k // 2) + 16 * (k % 2) + 8 * g
+            sums[k, g] = work.tile([P, 8, 32, PACK], F32, name="sums", tag="sums", bufs=3)
             nc.vector.tensor_tensor(
-                out=z[:],
-                in0=u_sb[:, 32 * b + i0 : 32 * b + i0 + 8, :].unsqueeze(2).to_broadcast([P, 8, 32, 4]),
-                in1=v_sb[:, 32 * b : 32 * b + 32, :].unsqueeze(1).to_broadcast([P, 8, 32, 4]),
+                out=sums[k, g][:],
+                in0=u_sb[:, i0 : i0 + 8, :].unsqueeze(2).to_broadcast([P, 8, 32, PACK]),
+                in1=v_sb[:, 32 * graph : 32 * graph + 32, :].unsqueeze(1).to_broadcast([P, 8, 32, PACK]),
                 op=ALU.add,
             )
-            zpre[k, g] = z
 
-        def e1_lrelu(k, g):
+        def lrelu_e1(e, k, g):
             if g == 0:
-                e1[k] = work.tile([P, 2048], BF16, name="e1", tag="e1", align_bytes=64)
-            z = zpre[k, g][:].rearrange("p i j t -> p (i j t)")
-            nc.vector.scalar_tensor_tensor(out=e1[k][:, 1024 * g : 1024 * g + 1024], in0=z, scalar=ALPHA, in1=z, op0=ALU.mult, op1=ALU.max)
+                e1[k] = work.tile([P, PAIRS * PACK], BF16, name="e1", tag="e1", align_bytes=64)
+            s = sums[k, g][:].rearrange("p i j t -> p (i j t)")
+            nc.vector.scalar_tensor_tensor(out=e1[k][:, 1024 * g : 1024 * g + 1024], in0=s, scalar=SLOPE, in1=s, op0=ALU.mult, op1=ALU.max)
 
-        def e1_quant(k, g0, g1):
-            if g0 == 0:
-                codes[k] = (
-                    work.tile([P, TOK], U32, name="e1_c", tag="e1_c", bufs=4, align_bytes=64),
-                    work.tile([P, TOK], U8, name="e1_s", tag="e1_s", bufs=4, align_bytes=64),
-                )
-            c, s = codes[k]
-            t0, t1 = 256 * g0, 256 * g1
-            nc.vector.quantize_mx(out=c[:, t0:t1].bitcast(FP8X4), scales=s[:, t0:t1], in_=e1[k][:, 4 * t0 : 4 * t1])
+        def quant_e1(e, k, r0, r1):
+            if r0 == 0:
+                codes[k] = work.tile([P, PAIRS], U32, name="codes", tag="codes", bufs=4, align_bytes=64)
+                scales[k] = work.tile([P, PAIRS], U8, name="scales", tag="scales", bufs=4, align_bytes=64)
+            nc.vector.quantize_mx(
+                out=codes[k][:, r0:r1].bitcast(FP8X4),
+                scales=scales[k][:, r0:r1],
+                in_=e1[k][:, PACK * r0 : PACK * r1],
+            )
 
-        acc = {}
-        at = {}
-        rt = {}
-        zp = {}
-        tp = {}
+        product = {}
+        lin = {}
+        pos = {}
+        biased = {}
+        turned = {}
 
-        def is_tok(n):
-            return n % 8 >= 8 - NP[n // 8]
+        def is_pair_tile(n):
+            return n % TILES >= TILES - PAIR_TILES[n // TILES]
 
-        def mx(n, t0, t1):
-            k, c = n // 8, n % 8
-            if t0 == 0:
-                acc[n] = psum.tile([P, TOK], F32, name="acc", tag="mm")
-            w_cols = slice(128 * c, 128 * c + 128)
-            if is_tok(n):
+        def width(half):
+            return 4 - (PAIR_TILES[half // 2] if half % 2 else 0)
+
+        def multiply(e, n, r0, r1):
+            k, c = n // TILES, n % TILES
+            ch = slice(P * c, P * c + P)
+            if r0 == 0:
+                product[n] = psum.tile([P, PAIRS], F32, name="product", tag="product")
+            if is_pair_tile(n):
                 for s in range(4):
+                    pairs = slice(P * s, P * s + P)
                     nc.tensor.matmul_mx(
-                        out=acc[n][:, 128 * s : 128 * s + 128],
-                        lhsT=codes[k][0][:, 128 * s : 128 * s + 128].bitcast(FP8X4),
-                        lhsT_scale=codes[k][1][:, 128 * s : 128 * s + 128],
-                        rhs=w1_c[:, w_cols].bitcast(FP8X4),
-                        rhs_scale=w1_s[:, w_cols],
+                        out=product[n][:, pairs],
+                        lhsT=codes[k][:, pairs].bitcast(FP8X4),
+                        lhsT_scale=scales[k][:, pairs],
+                        rhs=w1_codes[:, ch].bitcast(FP8X4),
+                        rhs_scale=w1_scales[:, ch],
                         start=True,
                         stop=True,
                     )
             else:
                 nc.tensor.matmul_mx(
-                    out=acc[n][:, t0:t1],
-                    lhsT=w1_c[:, w_cols].bitcast(FP8X4),
-                    lhsT_scale=w1_s[:, w_cols],
-                    rhs=codes[k][0][:, t0:t1].bitcast(FP8X4),
-                    rhs_scale=codes[k][1][:, t0:t1],
+                    out=product[n][:, r0:r1],
+                    lhsT=w1_codes[:, ch].bitcast(FP8X4),
+                    lhsT_scale=w1_scales[:, ch],
+                    rhs=codes[k][:, r0:r1].bitcast(FP8X4),
+                    rhs_scale=scales[k][:, r0:r1],
                     start=True,
                     stop=True,
                 )
 
-        def tok_add(n):
-            c = n % 8
-            zp[n] = work.tile([P, 4, P], F32, name="zp", tag="zp", bufs=3)
+        def add_b1(e, n):
+            c0 = P * (n % TILES) - F2 // 2
+            biased[n] = work.tile([P, 4, P], F32, name="biased", tag="biased", bufs=3)
             nc.vector.tensor_tensor(
-                out=zp[n][:],
-                in0=acc[n][:].rearrange("p (s c) -> p s c", s=4),
-                in1=b1_bc[:, 128 * c - 512 : 128 * c - 384].unsqueeze(1).to_broadcast([P, 4, P]),
+                out=biased[n][:],
+                in0=product[n][:].rearrange("p (s c) -> p s c", s=4),
+                in1=b1_wide[:, c0 : c0 + P].unsqueeze(1).to_broadcast([P, 4, P]),
                 op=ALU.add,
             )
 
-        def tok_lrelu(n):
-            k, c = n // 8, n % 8
-            o = work.tile([P, 4, P], F32, name="tok_o", tag="tok_o", bufs=3)
-            nc.vector.scalar_tensor_tensor(out=o[:], in0=zp[n][:], scalar=ALPHA, in1=zp[n][:], op0=ALU.mult, op1=ALU.max)
-            nc.sync.dma_start(out=rows[TOK * k : TOK * k + TOK, 128 * c : 128 * c + 128].rearrange("(s p) c -> p s c", p=P), in_=o[:])
+        def lrelu_out(e, n):
+            k, c = n // TILES, n % TILES
+            o = work.tile([P, 4, P], F32, name="o_pairs", tag="o_pairs", bufs=3)
+            nc.vector.scalar_tensor_tensor(out=o[:], in0=biased[n][:], scalar=SLOPE, in1=biased[n][:], op0=ALU.mult, op1=ALU.max)
+            nc.sync.dma_start(out=rows[PAIRS * k : PAIRS * k + PAIRS, P * c : P * c + P].rearrange("(s p) c -> p s c", p=P), in_=o[:])
 
-        def lin(n, t0, t1):
-            half, i = n // 4, n % 4
-            if i == 0 and t0 == 0:
-                at[half] = work.tile([P, 4, TOK], F32, name="at", tag="at", bufs=4)
-                rt[half] = work.tile([P, 4, TOK], F32, name="rt", tag="rt", bufs=4)
-            c = n % 8
-            nc.scalar.activation(out=at[half][:, i, t0:t1], in_=acc[n][:, t0:t1], func=ACT.Identity, bias=b1_a[:, c : c + 1], scale=ALPHA)
+        def linear(e, n, r0, r1):
+            half, i, c = n // 4, n % 4, n % TILES
+            if i == 0 and r0 == 0:
+                lin[half] = work.tile([P, 4, PAIRS], F32, name="lin", tag="lin", bufs=4)
+                pos[half] = work.tile([P, 4, PAIRS], F32, name="pos", tag="pos", bufs=4)
+            nc.scalar.activation(out=lin[half][:, i, r0:r1], in_=product[n][:, r0:r1], func=ACT.Identity, bias=b1_cols[:, c : c + 1], scale=SLOPE)
 
-        def relu(half, i0, i1):
-            nc.vector.tensor_scalar(out=rt[half][:, i0:i1, :], in0=at[half][:, i0:i1, :], scalar1=4.0, scalar2=0.0, op0=ALU.mult, op1=ALU.max)
+        def positive(e, half, i0, i1):
+            nc.vector.tensor_scalar(
+                out=pos[half][:, i0:i1, :],
+                in0=lin[half][:, i0:i1, :],
+                scalar1=(1.0 - SLOPE) / SLOPE,
+                scalar2=0.0,
+                op0=ALU.mult,
+                op1=ALU.max,
+            )
 
-        def tiles(half):
-            return 4 if half % 2 == 0 else 4 - NP[half // 2]
-
-        def turn(m):
+        def turn(e, m):
             half, s = m // 4, m % 4
-            tp[m] = psum.tile([P, TOK], F32, name="tp", tag="tp")
-            for i in range(tiles(half)):
-                for q, src in enumerate((at[half], rt[half])):
+            pairs = slice(P * s, P * s + P)
+            turned[m] = psum.tile([P, 4 * P], F32, name="turned", tag="turned")
+            for i in range(width(half)):
+                for part in (lin, pos):
                     nc.tensor.matmul(
-                        tp[m][:, 128 * i : 128 * i + 128],
-                        lhsT=src[:, i, 128 * s : 128 * s + 128],
+                        turned[m][:, P * i : P * i + P],
+                        lhsT=part[half][:, i, pairs],
                         rhs=ident[:],
                         is_transpose=True,
-                        start=(q == 0),
-                        stop=(q == 1),
+                        start=(part is lin),
+                        stop=(part is pos),
                     )
 
-        def leave(copy, m):
+        def leave(e, m):
             half, s = m // 4, m % 4
-            w = 128 * tiles(half)
-            o = work.tile([P, TOK], F32, name="o", tag="o", bufs=8)
-            copy(out=o[:, 0:w], in_=tp[m][:, 0:w])
-            r0, c0 = TOK * (half // 2) + 128 * s, 512 * (half % 2)
-            nc.sync.dma_start(out=rows[r0 : r0 + 128, c0 : c0 + w], in_=o[:, 0:w])
+            cols = P * width(half)
+            copy = nc.scalar.copy if e == "S" else nc.vector.tensor_copy
+            o = work.tile([P, 4 * P], F32, name="o", tag="o", bufs=12)
+            copy(out=o[:, 0:cols], in_=turned[m][:, 0:cols])
+            r0, c0 = PAIRS * (half // 2) + P * s, 4 * P * (half % 2)
+            nc.sync.dma_start(out=rows[r0 : r0 + P, c0 : c0 + cols], in_=o[:, 0:cols])
 
-        def half_tiles(n):
-            return n // 4, n % 4
+        queues = {}
 
-        lay_s, lay_v = nc.scalar.copy, nc.vector.tensor_copy
-        streams = {}
-
-        def item(stream, name, eng, cost, deps, fn, *args):
-            streams.setdefault(stream, []).append((name, eng, cost, deps, fn, args))
+        def step(queue, name, places, amount, after, call, *args):
+            queues.setdefault(queue, []).append((name, places, amount, after, call, args))
 
         for k in range(CHUNKS):
-            key = {"V": 8 * k - ELEAD}
-            parts = [("add", 0), ("lre", 0), ("q", 0), ("add", 1), ("lre", 1), ("q", 1)] if k == 0 else [("add", 0), ("add", 1), ("lre", 0), ("lre", 1), ("q", 1)]
-            for kind, g in parts:
-                if kind == "add":
-                    j = 2 * k + g - 3
-                    deps = ([("lre", j // 2, j % 2)] if j >= 0 else []) + (["v_rest", "u_rest"] if k >= 2 else [])
-                    item("e", ("add", k, g), key, 1040, deps, e1_add, k, g)
-                elif kind == "lre":
-                    deps = [("add", k, g)] + ([("q", k - 2, 1)] if k >= 2 else [])
-                    item("e", ("lre", k, g), key, 1040, deps, e1_lrelu, k, g)
+            place = {"V": TILES * k - E1_AHEAD}
+            by_half = [("sum", 0), ("lrelu", 0), ("codes", 0), ("sum", 1), ("lrelu", 1), ("codes", 1)]
+            by_kind = [("sum", 0), ("sum", 1), ("lrelu", 0), ("lrelu", 1), ("codes", 1)]
+            for kind, g in by_half if k == 0 else by_kind:
+                if kind == "sum":
+                    old = 2 * k + g - 3
+                    after = [("lrelu", old // 2, old % 2)] if old >= 0 else []
+                    step("e1", (kind, k, g), place, 1040, after + (["rest u", "rest v"] if k >= 2 else []), add_uv, k, g)
+                elif kind == "lrelu":
+                    after = [("codes", k - 2, 1)] if k >= 2 else []
+                    step("e1", (kind, k, g), place, 1040, after + [("sum", k, g)], lrelu_e1, k, g)
                 else:
-                    deps = [("lre", k, g)] + ([("mx", 8 * (k - 4) + 7, 1)] if k >= 4 else [])
-                    item("e", ("q", k, g), key, 560 if k else 290, deps, e1_quant, k, g if k == 0 else 0, g + 1)
+                    after = [("product", TILES * (k - 4) + TILES - 1, 1)] if k >= 4 else []
+                    r0, r1 = (256 * g, 256 * g + 256) if k == 0 else (0, PAIRS)
+                    step("e1", (kind, k, g), place, 560 if k else 290, after + [("lrelu", k, g)], quant_e1, k, r0, r1)
 
         for t in (2, 3):
-            item("w", ("wid", 0, t), {"S": -20}, 530, [], w1_widen, 0, t)
-        item("w", "lay0", {"S": -19}, 1180, [("wid", 0, 3)], w1_lay, lay_s, 0, 256)
-        item("w", "lay1", {"S": -19}, 1180, [("wid", 0, 3)], w1_lay, lay_s, 256, 512)
-        item("w", "b1", {"S": -19}, 30, [], b1_leave)
-        for t in range(4):
-            item("w", ("wid", 1, t), {"S": WKEY}, 530, [], w1_widen, 1, t)
-        item("w", "u_rest", {"S": UKEY}, 340, [], u_leave, 32, 128)
-        item("x", "wq0", {"V": -8}, 290, ["lay0"], w1_quant, 0, 256)
-        item("x", "wq1", {"V": -8}, 290, ["lay1"], w1_quant, 256, 512)
-        item("x", "lay2", {"V": LKEY}, 1280, [("wid", 1, 3)], w1_lay, lay_v, 512, 1024)
-        item("x", "wq2", {"V": LKEY}, 560, ["lay2"], w1_quant, 512, 1024)
-        item("v", "v_rest", {"V": UKEY}, 340, [], v_leave, 32, 128)
+            step("w1 first", ("wide 0", t), {"S": FIRST}, 530, [], widen_w1, t, 0, F2 // 2)
+        for q in range(2):
+            step("w1 first", ("laid", q), {"S": FIRST}, 1180, [("wide 0", 3)], lay_w1, 256 * q, 256 * q + 256)
+        step("w1 first", "b1", {"S": FIRST}, 30, [], leave_b1)
+        for t in range(PACK):
+            step("w1 wide", ("wide 1", t), {"V": FIRST}, 270, [], widen_w1, t, F2 // 2, F2)
+        step("rest u", "rest u", {"S": SOON}, 340, [], leave_u, 32, NODES)
+        for q in range(4):
+            if q >= 2:
+                step("w1 laid", ("laid", q), {"S": SOON}, 1180, [("wide 1", 3)], lay_w1, 256 * q, 256 * q + 256)
+            step("w1 codes", ("w1", q), {"V": 2 * q if q >= 2 else FIRST}, 280, [("laid", q)], quant_w1, 256 * q, 256 * q + 256)
+        step("rest v", "rest v", {"V": SOON}, 340, [], leave_v, 32, NODES)
 
-        for n in range(64):
-            k = n // 8
-            half, i = n // 4, n % 4
-            kind = "tok" if is_tok(n) else "lin"
+        for n in range(CHUNKS * TILES):
+            k, half, i = n // TILES, n // 4, n % 4
+            pair_tile = is_pair_tile(n)
             for g in (0, 1) if n < 4 else (1,):
-                t0, t1 = (256 * g, 256 * g + 256) if n < 4 else (0, 512)
-                deps = [("q", k, g), "wq0" if n < 2 else "wq1" if n < 4 else "wq2"]
+                r0, r1 = (256 * g, 256 * g + 256) if n < 4 else (0, PAIRS)
+                place = n + 2 * g if n < 4 else n
+                after = [("codes", k, g), ("w1", min(n // 2, 3))]
                 if n >= 4:
-                    deps.append(("tok" if is_tok(n - 4) else "lin", n - 4, 1))
-                if n < 4 and g == 1:
-                    deps.append(("lin", n, 0))
-                key = {"T": n - MXLEAD + (2 * g if n < 4 else 0)}
-                item("mx%d" % (g if n < 4 else 1), ("mx", n, g), key, 300 if kind == "tok" else 130 if n < 4 else 265, deps, mx, n, t0, t1)
-                if kind == "lin":
-                    deps = [("mx", n, g), "b1"] + ([("turn", 4 * half - 13)] if half >= 4 and i == 0 else [])
-                    item("lin%d" % (g if n < 4 else 1), ("lin", n, g), {"S": n + (2 * g if n < 4 else 0)}, 280 if n < 4 else 530, deps, lin, n, t0, t1)
-            if kind == "tok":
-                item("tok", ("tok", n, 1), {"V": n + P1LAG}, 530, [("mx", n, 1)], tok_add, n)
-                item("tok", ("tokl", n), {"V": n + P1LAG}, 530, [("tok", n, 1)], tok_lrelu, n)
-        for half in range(16):
-            w = tiles(half)
-            for i in range(0, w, 2):
-                j = min(i + 2, w)
-                item("relu", ("relu", half, j), {"V": 4 * half + j}, 20 + 256 * (j - i), [("lin", 4 * half + j - 1, 1)], relu, half, i, j)
-            for s in range(4):
-                m = 4 * half + s
-                item("turn", ("turn", m), {"T": m}, 160 * w, [("relu", half, w)] + ([("leave", m - 4)] if m >= 4 else []), turn, m)
-                item("leave", ("leave", m), {"S": m + COLAG, "V": m + VLAG}, 20 + 128 * w, [("turn", m)], leave, m)
+                    after.append(("read", n - 4, 1))
+                elif g == 1:
+                    after.append(("read", n, 0))
+                amount = 300 if pair_tile else 130 if n < 4 else 265
+                step("product %d" % g, ("product", n, g), {"T": place - MX_AHEAD}, amount, after, multiply, n, r0, r1)
+                if not pair_tile:
+                    after = [("product", n, g), "b1"] + ([("turned", 4 * half - 13)] if half >= 4 and i == 0 else [])
+                    step("linear %d" % g, ("read", n, g), {"S": place}, 280 if n < 4 else 530, after, linear, n, r0, r1)
+            if pair_tile:
+                step("pair tiles", ("read", n, 1), {"V": n}, 530, [("product", n, 1)], add_b1, n)
+                step("pair tiles", ("lrelu out", n), {"V": n}, 530, [("read", n, 1)], lrelu_out, n)
+        for half in range(2 * CHUNKS):
+            w = width(half)
+            for i0 in range(0, w, 2):
+                i1 = min(i0 + 2, w)
+                step("positive", ("positive", half, i1), {"V": 4 * half + i1}, 20 + 256 * (i1 - i0), [("read", 4 * half + i1 - 1, 1)], positive, half, i0, i1)
+            for m in range(4 * half, 4 * half + 4):
+                after = [("positive", half, w)] + ([("left", m - 4)] if m >= 4 else [])
+                step("turn", ("turned", m), {"T": m}, 2 * TURN * w, after, turn, m)
+                step("leave", ("left", m), {"S": m + LEAVE_S, "V": m + LEAVE_V}, 20 + P * w, [("turned", m)], leave, m)
 
         end = {}
-        ran = {}
-        clock = {"V": V0, "S": S0, "T": 0}
-        last = None
-        while any(streams.values()):
+        engine = {}
+        clock = {"V": 0, "S": S_BUSY, "T": 0}
+        last_call = None
+        while any(queues.values()):
             best = None
-            for st, queue in streams.items():
-                if not queue:
+            for queue, steps in queues.items():
+                if not steps:
                     continue
-                name, engs, cost, deps, fn, args = queue[0]
-                if not all(d in end for d in deps):
+                name, places, amount, after, call, args = steps[0]
+                if not all(a in end for a in after):
                     continue
-                for e, key in engs.items():
-                    start = max([clock[e]] + [end[d] + (SAME if ran[d] == e else HOP) for d in deps])
-                    rank = (start, key - (STICK if e == "T" and st[:2] == last else 0))
-                    if best is None or (e == best[1] and rank < best[0]) or (e != best[1] and start < best[0][0]):
-                        best = (rank, e, st)
-            rank, e, st = best
-            name, engs, cost, deps, fn, args = streams[st].pop(0)
-            if fn is leave:
-                fn(nc.scalar.copy if e == "S" else nc.vector.tensor_copy, *args)
-            else:
-                fn(*args)
-            clock[e] = rank[0] + cost
+                for e, place in places.items():
+                    start = max([clock[e]] + [end[a] + (AGAIN if engine[a] == e else HOP) for a in after])
+                    if e == "T" and call is last_call:
+                        place -= STAY
+                    if best is None or (e == best[2] and (start, place) < best[:2]) or (e != best[2] and start < best[0]):
+                        best = (start, place, e, queue)
+            start, place, e, queue = best
+            name, places, amount, after, call, args = queues[queue].pop(0)
+            call(e, *args)
+            clock[e] = start + amount
             if e == "T":
-                clock[e] += 100 if last is not None and last != st[:2] else 0
-                last = st[:2]
+                clock[e] += SWITCH if last_call is not None and call is not last_call else 0
+                last_call = call
             end[name] = clock[e]
-            ran[name] = e
+            engine[name] = e

from contextlib import ExitStack

import concourse.mybir as mybir
from concourse.masks import make_identity

F32 = mybir.dt.float32
BF16 = mybir.dt.bfloat16
U32 = mybir.dt.uint32
U8 = mybir.dt.uint8
FP8 = mybir.dt.float8_e4m3fn
FP8X4 = mybir.dt.float8_e4m3fn_x4
ALU = mybir.AluOpType
ACT = mybir.ActivationFunctionType

P = 128
NODES = 128
PACK = 4
K = P * PACK
F2 = 1024
PAIRS = 512
CHUNKS = 8
TILES = 8
SLOPE = 0.2

FLOPS = 2 * NODES * K * K * 2 + 2 * CHUNKS * PAIRS * K * F2

PAIR_TILES = (0, 1, 1, 0, 1, 1, 2, 3)

E1_AHEAD = 3.0
MX_AHEAD = 6.0
LEAVE_S = 6.0
LEAVE_V = 13.0
STAY = 1.0
FIRST = -20.0
SOON = 2.0
HOP = 75
AGAIN = 250
TURN = 80
SWITCH = 50
S_BUSY = 530


def tile_graph_gan_pa_kernel(tc, x, fe_w0, fe_b0, fe_w1_bytes, fe_w1_scale, fe_b1, out):
    nc = tc.nc
    rows = out.rearrange("b i j c -> (b i j) c")

    with ExitStack() as ctx:
        keep = ctx.enter_context(tc.tile_pool(name="keep", bufs=1))
        work = ctx.enter_context(tc.tile_pool(name="work", bufs=2))
        psum = ctx.enter_context(tc.psum_pool(name="psum", bufs=4))
        ctx.enter_context(tc.manual_schedule())

        w0_raw = [keep.tile([P, PACK, K], BF16, name="w0_raw%d" % h, align_bytes=64) for h in range(2)]
        x_sb = keep.tile([NODES, K], BF16, name="x_sb", align_bytes=64)
        w1_bytes = keep.tile([P, PACK * F2], U8, name="w1_bytes", align_bytes=64)
        w1_scale = keep.tile([P, PACK], F32, name="w1_scale")
        b0_sb = keep.tile([P, PACK], BF16, name="b0_sb")
        b1_rows = keep.tile([P, P], BF16, name="b1_rows")
        b1_wide = keep.tile([P, F2 // 2], BF16, name="b1_wide")

        def load_w0(h):
            nc.sync.dma_start(out=w0_raw[h][:], in_=fe_w0[K * h : K * h + K, :].rearrange("(p j) w -> p j w", j=PACK))

        load_w0(1)
        nc.sync.dma_start(out=x_sb[:], in_=x.rearrange("b n d -> (b n) d"))
        load_w0(0)
        nc.sync.dma_start(out=w1_bytes[:], in_=fe_w1_bytes.rearrange("(p t) n -> p (t n)", t=PACK))
        nc.scalar.dma_start(out=w1_scale[:], in_=fe_w1_scale.rearrange("(p t) o -> p (t o)", t=PACK))
        nc.scalar.dma_start(out=b0_sb[:], in_=fe_b0.rearrange("(p t) -> p t", t=PACK))

        ident = keep.tile([P, P], F32, name="ident")
        ident_bf16 = keep.tile([P, P], BF16, name="ident_bf16")
        warm = keep.tile([P, 8], F32, name="warm")
        nc.gpsimd.memset(warm[:], 0.0)
        nc.gpsimd.memset(b1_rows[:], 0.0)
        make_identity(nc, ident[:])
        make_identity(nc, ident_bf16[:])
        nc.sync.dma_start(out=b1_rows[0:TILES, :], in_=fe_b1.rearrange("(c m) -> c m", m=P))
        nc.sync.dma_start(out=b1_wide[:], in_=fe_b1[F2 // 2 : F2].partition_broadcast(P))
        nc.scalar.activation(out=warm[:], in_=warm[:], func=ACT.Identity, bias=0.0, scale=1.0)

        x_words = x_sb[:].bitcast(F32)
        x_turned = psum.tile([P, 2, NODES], F32, name="x_turned", tag="product")
        for w in range(2):
            nc.tensor.transpose(x_turned[:, w, :], x_words[:, w : K // 2 : 2], ident[:])
        x_laid = keep.tile([P, NODES, PACK], BF16, name="x_laid", align_bytes=64)
        x_codes = keep.tile([P, NODES], U32, name="x_codes", align_bytes=64)
        x_scales = keep.tile([P, NODES], U8, name="x_scales", align_bytes=64)

        w0_laid = [keep.tile([P, K * PACK], BF16, name="w0_laid%d" % h, align_bytes=64) for h in range(2)]
        w0_codes = [keep.tile([P, K], U32, name="w0_codes%d" % h, align_bytes=64) for h in range(2)]
        w0_scales = [keep.tile([P, K], U8, name="w0_scales%d" % h, align_bytes=64) for h in range(2)]

        def lay_w0(copy, h, t0, t1):
            copy(
                out=w0_laid[h][:].rearrange("p (t m j) -> p t m j", t=PACK, j=PACK)[:, t0:t1],
                in_=w0_raw[h][:].rearrange("p j (m t) -> p t m j", t=PACK)[:, t0:t1],
            )

        def quant_w0(h):
            nc.vector.quantize_mx(out=w0_codes[h][:].bitcast(FP8X4), scales=w0_scales[h][:], in_=w0_laid[h][:])

        lay_w0(nc.scalar.copy, 1, 2, 4)
        lay_w0(nc.vector.tensor_copy, 1, 0, 2)
        nc.vector.tensor_copy(
            out=x_laid[:].rearrange("p n t -> p (n t)").bitcast(F32).rearrange("p (n w) -> p n w", w=2),
            in_=x_turned[:].rearrange("p w n -> p n w"),
        )
        nc.vector.quantize_mx(out=x_codes[:].bitcast(FP8X4), scales=x_scales[:], in_=x_laid[:].rearrange("p n t -> p (n t)"))
        lay_w0(nc.vector.tensor_copy, 0, 0, 2)
        quant_w0(1)
        lay_w0(nc.scalar.copy, 0, 2, 4)
        quant_w0(0)

        w1_wide = keep.tile([P, PACK, F2], BF16, name="w1_wide", align_bytes=64)
        w1_laid = keep.tile([P, F2, PACK], BF16, name="w1_laid", align_bytes=64)
        w1_codes = keep.tile([P, F2], U32, name="w1_codes", align_bytes=64)
        w1_scales = keep.tile([P, F2], U8, name="w1_scales", align_bytes=64)

        def widen_w1(e, t, n0, n1):
            data = w1_bytes[:, F2 * t + n0 : F2 * t + n1].bitcast(FP8)
            scale = w1_scale[:, t : t + 1]
            if e == "S":
                nc.scalar.activation(out=w1_wide[:, t, n0:n1], in_=data, func=ACT.Copy, scale=scale)
            else:
                nc.vector.tensor_scalar(out=w1_wide[:, t, n0:n1], in0=data, scalar1=scale, scalar2=None, op0=ALU.mult)

        def lay_w1(e, n0, n1):
            nc.scalar.copy(
                out=w1_laid[:, n0:n1, :].rearrange("p (c i) t -> p c t i", i=4),
                in_=w1_wide[:, :, n0:n1].rearrange("p t (c i) -> p c t i", i=4),
            )

        def quant_w1(e, n0, n1):
            nc.vector.quantize_mx(
                out=w1_codes[:, n0:n1].bitcast(FP8X4),
                scales=w1_scales[:, n0:n1],
                in_=w1_laid[:, n0:n1, :].rearrange("p n t -> p (n t)"),
            )

        u_sb = keep.tile([P, NODES, PACK], F32, name="u_sb")
        v_sb = keep.tile([P, NODES, PACK], F32, name="v_sb")
        uv = {}

        def first_layer(h):
            uv[h] = psum.tile([P, PACK, NODES], F32, name="uv", tag="product")
            for t in range(PACK):
                nc.tensor.matmul_mx(
                    out=uv[h][:, t, :],
                    lhsT=w0_codes[h][:, P * t : P * t + P].bitcast(FP8X4),
                    lhsT_scale=w0_scales[h][:, P * t : P * t + P],
                    rhs=x_codes[:].bitcast(FP8X4),
                    rhs_scale=x_scales[:],
                    start=True,
                    stop=True,
                )

        def leave_u(e, n0, n1):
            nc.scalar.copy(out=u_sb[:, n0:n1, :], in_=uv[0][:, :, n0:n1].rearrange("p t n -> p n t"))

        def leave_v(e, n0, n1):
            nc.vector.tensor_tensor(
                out=v_sb[:, n0:n1, :],
                in0=uv[1][:, :, n0:n1].rearrange("p t n -> p n t"),
                in1=b0_sb[:].unsqueeze(1).to_broadcast([P, n1 - n0, PACK]),
                op=ALU.add,
            )

        widen_w1("S", 0, 0, F2 // 2)
        first_layer(1)
        first_layer(0)
        leave_v("V", 0, 32)
        widen_w1("S", 1, 0, F2 // 2)
        leave_u("S", 0, 32)

        b1_turned = psum.tile([P, P], BF16, name="b1_turned", tag="turned")
        nc.tensor.transpose(b1_turned[:], b1_rows[:], ident_bf16[:])
        b1_cols = keep.tile([P, TILES], F32, name="b1_cols")

        def leave_b1(e):
            nc.scalar.activation(out=b1_cols[:], in_=b1_turned[:, 0:TILES], func=ACT.Copy, scale=SLOPE)

        sums = {}
        e1 = {}
        codes = {}
        scales = {}

        def add_uv(e, k, g):
            graph, i0 = k // 2, 32 * (k // 2) + 16 * (k % 2) + 8 * g
            sums[k, g] = work.tile([P, 8, 32, PACK], F32, name="sums", tag="sums", bufs=3)
            nc.vector.tensor_tensor(
                out=sums[k, g][:],
                in0=u_sb[:, i0 : i0 + 8, :].unsqueeze(2).to_broadcast([P, 8, 32, PACK]),
                in1=v_sb[:, 32 * graph : 32 * graph + 32, :].unsqueeze(1).to_broadcast([P, 8, 32, PACK]),
                op=ALU.add,
            )

        def lrelu_e1(e, k, g):
            if g == 0:
                e1[k] = work.tile([P, PAIRS * PACK], BF16, name="e1", tag="e1", align_bytes=64)
            s = sums[k, g][:].rearrange("p i j t -> p (i j t)")
            nc.vector.scalar_tensor_tensor(out=e1[k][:, 1024 * g : 1024 * g + 1024], in0=s, scalar=SLOPE, in1=s, op0=ALU.mult, op1=ALU.max)

        def quant_e1(e, k, r0, r1):
            if r0 == 0:
                codes[k] = work.tile([P, PAIRS], U32, name="codes", tag="codes", bufs=4, align_bytes=64)
                scales[k] = work.tile([P, PAIRS], U8, name="scales", tag="scales", bufs=4, align_bytes=64)
            nc.vector.quantize_mx(
                out=codes[k][:, r0:r1].bitcast(FP8X4),
                scales=scales[k][:, r0:r1],
                in_=e1[k][:, PACK * r0 : PACK * r1],
            )

        product = {}
        lin = {}
        pos = {}
        biased = {}
        turned = {}

        def is_pair_tile(n):
            return n % TILES >= TILES - PAIR_TILES[n // TILES]

        def width(half):
            return 4 - (PAIR_TILES[half // 2] if half % 2 else 0)

        def multiply(e, n, r0, r1):
            k, c = n // TILES, n % TILES
            ch = slice(P * c, P * c + P)
            if r0 == 0:
                product[n] = psum.tile([P, PAIRS], F32, name="product", tag="product")
            if is_pair_tile(n):
                for s in range(4):
                    pairs = slice(P * s, P * s + P)
                    nc.tensor.matmul_mx(
                        out=product[n][:, pairs],
                        lhsT=codes[k][:, pairs].bitcast(FP8X4),
                        lhsT_scale=scales[k][:, pairs],
                        rhs=w1_codes[:, ch].bitcast(FP8X4),
                        rhs_scale=w1_scales[:, ch],
                        start=True,
                        stop=True,
                    )
            else:
                nc.tensor.matmul_mx(
                    out=product[n][:, r0:r1],
                    lhsT=w1_codes[:, ch].bitcast(FP8X4),
                    lhsT_scale=w1_scales[:, ch],
                    rhs=codes[k][:, r0:r1].bitcast(FP8X4),
                    rhs_scale=scales[k][:, r0:r1],
                    start=True,
                    stop=True,
                )

        def add_b1(e, n):
            c0 = P * (n % TILES) - F2 // 2
            biased[n] = work.tile([P, 4, P], F32, name="biased", tag="biased", bufs=3)
            nc.vector.tensor_tensor(
                out=biased[n][:],
                in0=product[n][:].rearrange("p (s c) -> p s c", s=4),
                in1=b1_wide[:, c0 : c0 + P].unsqueeze(1).to_broadcast([P, 4, P]),
                op=ALU.add,
            )

        def lrelu_out(e, n):
            k, c = n // TILES, n % TILES
            o = work.tile([P, 4, P], F32, name="o_pairs", tag="o_pairs", bufs=3)
            nc.vector.scalar_tensor_tensor(out=o[:], in0=biased[n][:], scalar=SLOPE, in1=biased[n][:], op0=ALU.mult, op1=ALU.max)
            nc.sync.dma_start(out=rows[PAIRS * k : PAIRS * k + PAIRS, P * c : P * c + P].rearrange("(s p) c -> p s c", p=P), in_=o[:])

        def linear(e, n, r0, r1):
            half, i, c = n // 4, n % 4, n % TILES
            if i == 0 and r0 == 0:
                lin[half] = work.tile([P, 4, PAIRS], F32, name="lin", tag="lin", bufs=4)
                pos[half] = work.tile([P, 4, PAIRS], F32, name="pos", tag="pos", bufs=4)
            nc.scalar.activation(out=lin[half][:, i, r0:r1], in_=product[n][:, r0:r1], func=ACT.Identity, bias=b1_cols[:, c : c + 1], scale=SLOPE)

        def positive(e, half, i0, i1):
            nc.vector.tensor_scalar(
                out=pos[half][:, i0:i1, :],
                in0=lin[half][:, i0:i1, :],
                scalar1=(1.0 - SLOPE) / SLOPE,
                scalar2=0.0,
                op0=ALU.mult,
                op1=ALU.max,
            )

        def turn(e, m):
            half, s = m // 4, m % 4
            pairs = slice(P * s, P * s + P)
            turned[m] = psum.tile([P, 4 * P], F32, name="turned", tag="turned")
            for i in range(width(half)):
                for part in (lin, pos):
                    nc.tensor.matmul(
                        turned[m][:, P * i : P * i + P],
                        lhsT=part[half][:, i, pairs],
                        rhs=ident[:],
                        is_transpose=True,
                        start=(part is lin),
                        stop=(part is pos),
                    )

        def leave(e, m):
            half, s = m // 4, m % 4
            cols = P * width(half)
            copy = nc.scalar.copy if e == "S" else nc.vector.tensor_copy
            o = work.tile([P, 4 * P], F32, name="o", tag="o", bufs=12)
            copy(out=o[:, 0:cols], in_=turned[m][:, 0:cols])
            r0, c0 = PAIRS * (half // 2) + P * s, 4 * P * (half % 2)
            nc.sync.dma_start(out=rows[r0 : r0 + P, c0 : c0 + cols], in_=o[:, 0:cols])

        queues = {}

        def step(queue, name, places, amount, after, call, *args):
            queues.setdefault(queue, []).append((name, places, amount, after, call, args))

        for k in range(CHUNKS):
            place = {"V": TILES * k - E1_AHEAD}
            by_half = [("sum", 0), ("lrelu", 0), ("codes", 0), ("sum", 1), ("lrelu", 1), ("codes", 1)]
            by_kind = [("sum", 0), ("sum", 1), ("lrelu", 0), ("lrelu", 1), ("codes", 1)]
            for kind, g in by_half if k == 0 else by_kind:
                if kind == "sum":
                    old = 2 * k + g - 3
                    after = [("lrelu", old // 2, old % 2)] if old >= 0 else []
                    step("e1", (kind, k, g), place, 1040, after + (["rest u", "rest v"] if k >= 2 else []), add_uv, k, g)
                elif kind == "lrelu":
                    after = [("codes", k - 2, 1)] if k >= 2 else []
                    step("e1", (kind, k, g), place, 1040, after + [("sum", k, g)], lrelu_e1, k, g)
                else:
                    after = [("product", TILES * (k - 4) + TILES - 1, 1)] if k >= 4 else []
                    r0, r1 = (256 * g, 256 * g + 256) if k == 0 else (0, PAIRS)
                    step("e1", (kind, k, g), place, 560 if k else 290, after + [("lrelu", k, g)], quant_e1, k, r0, r1)

        for t in (2, 3):
            step("w1 first", ("wide 0", t), {"S": FIRST}, 530, [], widen_w1, t, 0, F2 // 2)
        for q in range(2):
            step("w1 first", ("laid", q), {"S": FIRST}, 1180, [("wide 0", 3)], lay_w1, 256 * q, 256 * q + 256)
        step("w1 first", "b1", {"S": FIRST}, 30, [], leave_b1)
        for t in range(PACK):
            step("w1 wide", ("wide 1", t), {"V": FIRST}, 270, [], widen_w1, t, F2 // 2, F2)
        step("rest u", "rest u", {"S": SOON}, 340, [], leave_u, 32, NODES)
        for q in range(4):
            if q >= 2:
                step("w1 laid", ("laid", q), {"S": SOON}, 1180, [("wide 1", 3)], lay_w1, 256 * q, 256 * q + 256)
            step("w1 codes", ("w1", q), {"V": 2 * q if q >= 2 else FIRST}, 280, [("laid", q)], quant_w1, 256 * q, 256 * q + 256)
        step("rest v", "rest v", {"V": SOON}, 340, [], leave_v, 32, NODES)

        for n in range(CHUNKS * TILES):
            k, half, i = n // TILES, n // 4, n % 4
            pair_tile = is_pair_tile(n)
            for g in (0, 1) if n < 4 else (1,):
                r0, r1 = (256 * g, 256 * g + 256) if n < 4 else (0, PAIRS)
                place = n + 2 * g if n < 4 else n
                after = [("codes", k, g), ("w1", min(n // 2, 3))]
                if n >= 4:
                    after.append(("read", n - 4, 1))
                elif g == 1:
                    after.append(("read", n, 0))
                amount = 300 if pair_tile else 130 if n < 4 else 265
                step("product %d" % g, ("product", n, g), {"T": place - MX_AHEAD}, amount, after, multiply, n, r0, r1)
                if not pair_tile:
                    after = [("product", n, g), "b1"] + ([("turned", 4 * half - 13)] if half >= 4 and i == 0 else [])
                    step("linear %d" % g, ("read", n, g), {"S": place}, 280 if n < 4 else 530, after, linear, n, r0, r1)
            if pair_tile:
                step("pair tiles", ("read", n, 1), {"V": n}, 530, [("product", n, 1)], add_b1, n)
                step("pair tiles", ("lrelu out", n), {"V": n}, 530, [("read", n, 1)], lrelu_out, n)
        for half in range(2 * CHUNKS):
            w = width(half)
            for i0 in range(0, w, 2):
                i1 = min(i0 + 2, w)
                step("positive", ("positive", half, i1), {"V": 4 * half + i1}, 20 + 256 * (i1 - i0), [("read", 4 * half + i1 - 1, 1)], positive, half, i0, i1)
            for m in range(4 * half, 4 * half + 4):
                after = [("positive", half, w)] + ([("left", m - 4)] if m >= 4 else [])
                step("turn", ("turned", m), {"T": m}, 2 * TURN * w, after, turn, m)
                step("leave", ("left", m), {"S": m + LEAVE_S, "V": m + LEAVE_V}, 20 + P * w, [("turned", m)], leave, m)

        end = {}
        engine = {}
        clock = {"V": 0, "S": S_BUSY, "T": 0}
        last_call = None
        while any(queues.values()):
            best = None
            for queue, steps in queues.items():
                if not steps:
                    continue
                name, places, amount, after, call, args = steps[0]
                if not all(a in end for a in after):
                    continue
                for e, place in places.items():
                    start = max([clock[e]] + [end[a] + (AGAIN if engine[a] == e else HOP) for a in after])
                    if e == "T" and call is last_call:
                        place -= STAY
                    if best is None or (e == best[2] and (start, place) < best[:2]) or (e != best[2] and start < best[0]):
                        best = (start, place, e, queue)
            start, place, e, queue = best
            name, places, amount, after, call, args = queues[queue].pop(0)
            call(e, *args)
            clock[e] = start + amount
            if e == "T":
                clock[e] += SWITCH if last_call is not None and call is not last_call else 0
                last_call = call
            end[name] = clock[e]
            engine[name] = e
